import numpy as np
import ml_dtypes


def mxq(x, axis, fmt="e4m3"):
    dtype, down = {"e4m3": (ml_dtypes.float8_e4m3fn, 7), "e5m2": (ml_dtypes.float8_e5m2, 14)}[fmt]
    v = np.moveaxis(np.asarray(x, np.float32).astype(ml_dtypes.bfloat16).astype(np.float64), axis, -1)
    blocks = v.reshape(v.shape[:-1] + (-1, 32))
    amax = np.abs(blocks).max(-1, keepdims=True)
    byte = np.maximum(np.where(amax > 0, np.frexp(amax)[1] - 1 + 127, 0) - down, 1)
    scale = np.exp2(byte - 127.0)
    codes = (blocks / scale).astype(np.float32).astype(dtype).astype(np.float64)
    return np.moveaxis((codes * scale).reshape(v.shape), -1, axis)


WIDE = False


def mx_kscale(k):
    if not WIDE:
        return np.ones(k)
    levels = np.array([10, -10, 5, -5, 0])
    a = np.random.permutation(np.resize(levels, k // 512 * 4)).reshape(k // 512, 4)
    idx = np.arange(k)
    return np.exp2(a[idx // 512, idx % 128 // 32])


BF16 = ml_dtypes.bfloat16


def bf(x):
    return np.asarray(x, np.float32).astype(BF16)


def f64(x):
    return np.asarray(x).astype(np.float64)


E2M1 = np.array([0.0, 0.5, 1.0, 1.5, 2.0, 3.0, 4.0, 6.0, -0.0, -0.5, -1.0, -1.5, -2.0, -3.0, -4.0, -6.0])


def pack_weight(w, fmt):
    k, n = w.shape
    w = f64(bf(w)).reshape(k // 32, 32, n)
    amax = np.abs(w).max(1)
    if fmt == "e4m3":
        byte = np.frexp(amax)[1] - 1 + 127 - 7
    else:
        mant, ex = np.frexp(amax / 6.0)
        byte = np.where(mant > 0.5, ex, ex - 1) + 127
    byte = np.clip(np.where(amax > 0, byte, 1), 1, 254)
    scaled = (w * np.exp2(127.0 - byte)[:, None, :]).reshape(k, n).astype(np.float32)
    by_word = np.ascontiguousarray(scaled.reshape(k // 512, 128, 4, n).transpose(0, 1, 3, 2))
    if fmt == "e4m3":
        words = by_word.astype(ml_dtypes.float8_e4m3fn).view(np.uint8)
    else:
        c = by_word.astype(ml_dtypes.float4_e2m1fn).view(np.uint8) & 0xF
        words = c[..., 0::2] | (c[..., 1::2] << 4)
    return np.ascontiguousarray(words), np.ascontiguousarray(byte.astype(np.uint8).reshape(k // 512, 16, n))


def unpack_weight(words, scales, fmt):
    g, p, n, _ = words.shape
    if fmt == "e4m3":
        vals = np.ascontiguousarray(words).view(ml_dtypes.float8_e4m3fn).astype(np.float64)
    else:
        nib = np.empty((g, p, n, 4), np.uint8)
        nib[..., 0::2] = words & 0xF
        nib[..., 1::2] = words >> 4
        vals = E2M1[nib]
    vals = vals * np.repeat(np.exp2(scales.astype(np.float64) - 127.0), 8, axis=1)[..., None]
    return vals.transpose(0, 1, 3, 2).reshape(g * 512, n)

def pack4(w):
    words, scales = pack_weight(w, "e2m1")
    return words.reshape(words.shape[0], 128, -1), scales


def unpack4(words, scales):
    return unpack_weight(words.reshape(words.shape[0], 128, -1, 2), scales, "e2m1")


B, T, D, NH, HD, G, RD, F = 1, 640, 1024, 8, 1024, 2, 16, 4096
HKV = NH // G
C = NH * HD


def setup_inputs():
    s = mx_kscale(C).reshape(NH, HD)
    sh = np.where(np.arange(NH) % 2 == 0, s.max(axis=1), s.min(axis=1))
    v = np.random.standard_normal((B, HKV, T, HD))
    a = 0.4 * np.random.standard_normal((B, HKV, G, T, HD)) + 0.4 * v[:, :, None]
    x = bf(np.random.standard_normal((B, T, D)) * np.random.uniform(0.5, 2.0, (B, T, 1)))
    wo = np.random.standard_normal((D, C)) / np.sqrt(C) / np.repeat(sh, HD)[None, :]
    wo_words, wo_scales = pack4(np.ascontiguousarray(wo.T))
    return {"attn_out": bf(a * sh.reshape(HKV, G)[None, :, :, None, None]),
            "v": bf(v),
            "x": x,
            "wo_words": wo_words,
            "wo_scales": wo_scales,
            "attn_scale": bf(1.0 + 0.1 * np.random.standard_normal(D))}


def reference(attn_out, v, x, wo_words, wo_scales, attn_scale):
    y_g = f64(attn_out).transpose(0, 3, 1, 2, 4)
    v_t = f64(v).transpose(0, 2, 1, 3)
    vn = v_t / np.maximum(np.sqrt(np.sum(np.square(v_t), axis=-1, keepdims=True)), 1e-12)
    vn = vn[:, :, :, None, :]
    proj = np.sum(y_g * vn, axis=-1, keepdims=True) * vn
    y = (y_g - proj).reshape(B, T, C)
    return f64(x) + f64(attn_scale) * (mxq(y, 2, "e4m3") @ unpack4(wo_words, wo_scales))

@@ -1,0 +1,251 @@
+from contextlib import ExitStack
+
+import concourse.mybir as mybir
+from concourse.masks import make_identity
+
+BF16 = mybir.dt.bfloat16
+F32 = mybir.dt.float32
+I32 = mybir.dt.int32
+U32 = mybir.dt.uint32
+U8 = mybir.dt.uint8
+FP8X4 = mybir.dt.float8_e4m3fn_x4
+FP4X4 = mybir.dt.float4_e2m1fn_x4
+ALU = mybir.AluOpType
+ACT = mybir.ActivationFunctionType
+
+P = 128
+TOKENS = 640
+KV_HEADS = 4
+GROUP = 2
+HEAD_DIM = 1024
+D_OUT = 1024
+NORM_FLOOR = 1e-12
+
+PACK = 4
+K_PASS = P * PACK
+HEAD_PASSES = HEAD_DIM // K_PASS
+UNIT_PASSES = GROUP * HEAD_PASSES
+PASSES = KV_HEADS * UNIT_PASSES
+N_BANK = 512
+N_BANKS = D_OUT // N_BANK
+PAIR = 2
+HALVES = PACK // PAIR
+QUADRANTS = 4
+LIVE_ROWS = 4
+
+TOKEN_TILES = TOKENS // P
+UNITS = TOKEN_TILES * KV_HEADS
+LOOKAHEAD = 3
+
+FLOPS = 2 * TOKENS * KV_HEADS * GROUP * HEAD_DIM * D_OUT
+
+
+def tile_block_pb_k_kernel(tc, attn_out, v, x, wo_words, wo_scales, attn_scale, out):
+    nc = tc.nc
+    with ExitStack() as ctx:
+        consts = ctx.enter_context(tc.tile_pool(name="consts", bufs=1))
+        inputs = ctx.enter_context(tc.tile_pool(name="inputs", bufs=LOOKAHEAD + 1))
+        work = ctx.enter_context(tc.tile_pool(name="work", bufs=2))
+        small = ctx.enter_context(tc.tile_pool(name="small", bufs=4))
+        psum_t = ctx.enter_context(tc.psum_pool(name="psum_t", bufs=2))
+        psum_acc = ctx.enter_context(tc.psum_pool(name="psum_acc", bufs=2))
+        ctx.enter_context(tc.manual_schedule())
+
+        tiles = {}
+
+        identity = consts.tile([P, P], F32, name="identity")
+        make_identity(nc, identity[:])
+
+        w_words = consts.tile([P, PASSES, PAIR * D_OUT], U8, name="w_words", align_bytes=64)
+        w_planes = consts.tile([P, PASSES, D_OUT], U8, name="w_planes", align_bytes=64)
+        nc.vector.memset(w_planes[:].bitcast(I32), 0)
+        gain = consts.tile([P, D_OUT], BF16, name="gain")
+
+        def in_range(j):
+            return 0 <= j < UNITS
+
+        def load_weights(h):
+            passes = slice(h * UNIT_PASSES, (h + 1) * UNIT_PASSES)
+            nc.sync.dma_start(
+                out=w_words[:, passes, :].bitcast(I32),
+                in_=wo_words[passes].rearrange("c p b -> p c b").bitcast(I32),
+            )
+            for quadrant in range(QUADRANTS):
+                rows = slice(quadrant * LIVE_ROWS, (quadrant + 1) * LIVE_ROWS)
+                first = quadrant * (P // QUADRANTS)
+                nc.sync.dma_start(
+                    out=w_planes[first : first + LIVE_ROWS, passes, :].bitcast(I32),
+                    in_=wo_scales[passes, rows, :].rearrange("c r n -> r c n").bitcast(I32),
+                )
+
+        def load(j):
+            if not in_range(j):
+                return
+            i, h = divmod(j, KV_HEADS)
+            tokens = slice(i * P, (i + 1) * P)
+            v_sb = inputs.tile([P, HEAD_DIM], BF16, name="v_sb", tag="v_sb")
+            nc.sync.dma_start(out=v_sb[:], in_=v[0, h, tokens, :])
+            a_sb = inputs.tile([P, GROUP, HEAD_DIM], BF16, name="a_sb", tag="a_sb")
+            nc.sync.dma_start(
+                out=a_sb[:], in_=attn_out[0, h, :, tokens, :].rearrange("g p d -> p g d")
+            )
+            tiles["v", j] = v_sb
+            tiles["a", j] = a_sb
+            if i == 0:
+                load_weights(h)
+            if h == 0:
+                x_sb = inputs.tile([P, D_OUT], BF16, name="x_sb", tag="x_sb")
+                nc.sync.dma_start(out=x_sb[:], in_=x[0, tokens, :])
+                tiles["x", i] = x_sb
+
+        def square_sum(j):
+            if not in_range(j):
+                return
+            squares = work.tile([P, HEAD_DIM], BF16, name="squares", tag="squares")
+            ssq = small.tile([P, 1], F32, name="ssq", tag="ssq")
+            nc.scalar.activation(
+                out=squares[:], in_=tiles["v", j][:], func=ACT.Square, accum_out=ssq[:]
+            )
+            tiles["ssq", j] = ssq
+
+        def clamp(j):
+            if not in_range(j):
+                return
+            neg_ssq = small.tile([P, 1], F32, name="neg_ssq", tag="neg_ssq")
+            nc.vector.tensor_scalar(
+                out=neg_ssq[:],
+                in0=tiles["ssq", j][:],
+                scalar1=NORM_FLOOR * NORM_FLOOR,
+                scalar2=-1.0,
+                op0=ALU.max,
+                op1=ALU.mult,
+            )
+            tiles["neg_ssq", j] = neg_ssq
+
+        def invert(j):
+            if not in_range(j):
+                return
+            neg_inv = small.tile([P, 1], F32, name="neg_inv", tag="neg_inv")
+            nc.vector.reciprocal(out=neg_inv[:], in_=tiles["neg_ssq", j][:])
+            tiles["neg_inv", j] = neg_inv
+
+        def dot(j, g):
+            if g == 0:
+                tiles["neg_c", j] = small.tile([P, GROUP], F32, name="neg_c", tag="neg_c")
+            products = work.tile([P, HEAD_DIM], BF16, name="products", tag="products")
+            nc.vector.scalar_tensor_tensor(
+                out=products[:],
+                in0=tiles["a", j][:, g, :],
+                scalar=tiles["neg_inv", j][:, 0:1],
+                in1=tiles["v", j][:],
+                op0=ALU.mult,
+                op1=ALU.mult,
+                accum_out=tiles["neg_c", j][:, g : g + 1],
+            )
+
+        def subtract(j, g):
+            if g == 0:
+                tiles["y", j] = work.tile([P, GROUP, HEAD_DIM], BF16, name="y_sb", tag="y_sb")
+            nc.vector.scalar_tensor_tensor(
+                out=tiles["y", j][:, g, :],
+                in0=tiles["v", j][:],
+                scalar=tiles["neg_c", j][:, g : g + 1],
+                in1=tiles["a", j][:, g, :],
+                op0=ALU.mult,
+                op1=ALU.add,
+            )
+
+        def transpose(j, g):
+            if g == 0:
+                tiles["grouped", j] = work.tile(
+                    [P, GROUP, PACK * HEAD_PASSES * P], BF16, name="grouped", tag="grouped", align_bytes=64
+                )
+            y_words = tiles["y", j][:, g, :].bitcast(F32)
+            turned = psum_t.tile([P, HALVES, HEAD_PASSES * P], F32, name="turned", tag="turned%d" % g)
+            pass_words = K_PASS // PAIR
+            for c in range(HEAD_PASSES):
+                for u in range(HALVES):
+                    nc.tensor.transpose(
+                        turned[:, u, c * P : (c + 1) * P],
+                        y_words[:, c * pass_words + u : (c + 1) * pass_words : HALVES],
+                        identity[:],
+                    )
+            nc.scalar.copy(
+                out=tiles["grouped", j][:, g, :].bitcast(F32).rearrange("p (q u) -> p q u", u=HALVES),
+                in_=turned[:].rearrange("p u q -> p q u"),
+            )
+
+        def quantise(j):
+            if not in_range(j):
+                return
+            y_codes = work.tile([P, UNIT_PASSES * P], U32, name="y_codes", tag="y_codes", align_bytes=64)
+            y_planes = work.tile([P, UNIT_PASSES * P], U8, name="y_planes", tag="y_planes", align_bytes=64)
+            nc.vector.quantize_mx(
+                out=y_codes[:].bitcast(FP8X4),
+                scales=y_planes[:],
+                in_=tiles["grouped", j][:].rearrange("p g c -> p (g c)"),
+            )
+            tiles["y_codes", j] = y_codes
+            tiles["y_planes", j] = y_planes
+
+        def multiply(j):
+            if not in_range(j):
+                return
+            i, h = divmod(j, KV_HEADS)
+            if h == 0:
+                for b in range(N_BANKS):
+                    tiles["acc%d" % b, i] = psum_acc.tile([P, N_BANK], F32, name="acc", tag="acc%d" % b)
+            for c in range(UNIT_PASSES):
+                w_pass = h * UNIT_PASSES + c
+                token_cols = slice(c * P, (c + 1) * P)
+                for b in range(N_BANKS):
+                    nc.tensor.matmul_mx(
+                        out=tiles["acc%d" % b, i][:],
+                        lhsT=tiles["y_codes", j][:, token_cols].bitcast(FP8X4),
+                        lhsT_scale=tiles["y_planes", j][:, token_cols],
+                        rhs=w_words[:, w_pass, b * PAIR * N_BANK : (b + 1) * PAIR * N_BANK].bitcast(FP4X4),
+                        rhs_scale=w_planes[:, w_pass, b * N_BANK : (b + 1) * N_BANK],
+                        start=(w_pass == 0),
+                        stop=(w_pass == PASSES - 1),
+                    )
+
+        def finish(j):
+            i, h = divmod(j, KV_HEADS)
+            if not in_range(j) or h != KV_HEADS - 1:
+                return
+            scaled = work.tile([P, D_OUT], F32, name="scaled", tag="scaled")
+            result = work.tile([P, D_OUT], F32, name="result", tag="result")
+            for b in range(N_BANKS):
+                cols = slice(b * N_BANK, (b + 1) * N_BANK)
+                nc.vector.tensor_tensor(
+                    out=scaled[:, cols], in0=tiles["acc%d" % b, i][:], in1=gain[:, cols], op=ALU.mult
+                )
+            for b in range(N_BANKS):
+                cols = slice(b * N_BANK, (b + 1) * N_BANK)
+                nc.vector.tensor_tensor(
+                    out=result[:, cols], in0=scaled[:, cols], in1=tiles["x", i][:, cols], op=ALU.add
+                )
+            nc.sync.dma_start(out=out[0, i * P : (i + 1) * P, :], in_=result[:])
+
+        for j in range(LOOKAHEAD):
+            load(j)
+        nc.sync.dma_start(out=gain[:], in_=attn_scale.partition_broadcast(P))
+        square_sum(0)
+        square_sum(1)
+        clamp(0)
+        invert(0)
+
+        for s in range(UNITS + 2):
+            load(s + LOOKAHEAD)
+            if in_range(s):
+                dot(s, 0)
+                clamp(s + 1)
+                dot(s, 1)
+                invert(s + 1)
+                for g in range(GROUP):
+                    subtract(s, g)
+                    transpose(s, g)
+                square_sum(s + 2)
+            quantise(s - 1)
+            multiply(s - 1)
+            finish(s - 2)

@@ -36,6 +36,8 @@ LIVE_ROWS = 4
 TOKEN_TILES = TOKENS // P
 UNITS = TOKEN_TILES * KV_HEADS
 LOOKAHEAD = 3
+VECTOR_HEAD = 0
+POOL_HEAD = 1
 
 FLOPS = 2 * TOKENS * KV_HEADS * GROUP * HEAD_DIM * D_OUT
 
@@ -44,10 +46,11 @@ def tile_block_pb_k_kernel(tc, attn_out, v, x, wo_words, wo_scales, attn_scale, 
     nc = tc.nc
     with ExitStack() as ctx:
         consts = ctx.enter_context(tc.tile_pool(name="consts", bufs=1))
-        inputs = ctx.enter_context(tc.tile_pool(name="inputs", bufs=LOOKAHEAD + 1))
+        inputs = ctx.enter_context(tc.tile_pool(name="inputs", bufs=LOOKAHEAD + 2))
         work = ctx.enter_context(tc.tile_pool(name="work", bufs=2))
         small = ctx.enter_context(tc.tile_pool(name="small", bufs=4))
-        psum_t = ctx.enter_context(tc.psum_pool(name="psum_t", bufs=2))
+        psum_v = ctx.enter_context(tc.psum_pool(name="psum_v", bufs=2))
+        psum_t = ctx.enter_context(tc.psum_pool(name="psum_t", bufs=1))
         psum_acc = ctx.enter_context(tc.psum_pool(name="psum_acc", bufs=2))
         ctx.enter_context(tc.manual_schedule())
 
@@ -55,6 +58,8 @@ def tile_block_pb_k_kernel(tc, attn_out, v, x, wo_words, wo_scales, attn_scale, 
 
         identity = consts.tile([P, P], F32, name="identity")
         make_identity(nc, identity[:])
+        identity_bf = consts.tile([P, P], BF16, name="identity_bf")
+        make_identity(nc, identity_bf[:])
 
         w_words = consts.tile([P, PASSES, PAIR * D_OUT], U8, name="w_words", align_bytes=64)
         w_planes = consts.tile([P, PASSES, D_OUT], U8, name="w_planes", align_bytes=64)
@@ -91,10 +96,8 @@ def tile_block_pb_k_kernel(tc, attn_out, v, x, wo_words, wo_scales, attn_scale, 
             )
             tiles["v", j] = v_sb
             tiles["a", j] = a_sb
-            if i == 0:
-                load_weights(h)
-            if h == 0:
-                x_sb = inputs.tile([P, D_OUT], BF16, name="x_sb", tag="x_sb")
+            if h == KV_HEADS - 1:
+                x_sb = work.tile([P, D_OUT], BF16, name="x_sb", tag="x_sb")
                 nc.sync.dma_start(out=x_sb[:], in_=x[0, tokens, :])
                 tiles["x", i] = x_sb
 
@@ -107,6 +110,17 @@ def tile_block_pb_k_kernel(tc, attn_out, v, x, wo_words, wo_scales, attn_scale, 
                 out=squares[:], in_=tiles["v", j][:], func=ACT.Square, accum_out=ssq[:]
             )
             tiles["ssq", j] = ssq
+
+        def mirror(j):
+            if not in_range(j):
+                return
+            v_ps = psum_v.tile([P, HEAD_DIM], BF16, name="v_ps", tag="v_ps")
+            for b in range(HEAD_DIM // N_BANK):
+                cols = slice(b * N_BANK, (b + 1) * N_BANK)
+                nc.tensor.matmul(
+                    out=v_ps[:, cols], lhsT=identity_bf[:], rhs=tiles["v", j][:, cols], start=True, stop=True
+                )
+            tiles["v_ps", j] = v_ps
 
         def clamp(j):
             if not in_range(j):
@@ -130,37 +144,62 @@ def tile_block_pb_k_kernel(tc, attn_out, v, x, wo_words, wo_scales, attn_scale, 
             tiles["neg_inv", j] = neg_inv
 
         def dot(j, g):
-            if g == 0:
+            if g == VECTOR_HEAD:
                 tiles["neg_c", j] = small.tile([P, GROUP], F32, name="neg_c", tag="neg_c")
             products = work.tile([P, HEAD_DIM], BF16, name="products", tag="products")
             nc.vector.scalar_tensor_tensor(
                 out=products[:],
                 in0=tiles["a", j][:, g, :],
                 scalar=tiles["neg_inv", j][:, 0:1],
-                in1=tiles["v", j][:],
+                in1=tiles["v_ps", j][:],
                 op0=ALU.mult,
                 op1=ALU.mult,
                 accum_out=tiles["neg_c", j][:, g : g + 1],
             )
 
-        def subtract(j, g):
-            if g == 0:
-                tiles["y", j] = work.tile([P, GROUP, HEAD_DIM], BF16, name="y_sb", tag="y_sb")
+        def subtract(j):
+            g = VECTOR_HEAD
+            y_sb = work.tile([P, HEAD_DIM], BF16, name="y_sb", tag="y_sb%d" % g)
             nc.vector.scalar_tensor_tensor(
-                out=tiles["y", j][:, g, :],
-                in0=tiles["v", j][:],
+                out=y_sb[:],
+                in0=tiles["v_ps", j][:],
                 scalar=tiles["neg_c", j][:, g : g + 1],
                 in1=tiles["a", j][:, g, :],
                 op0=ALU.mult,
                 op1=ALU.add,
             )
+            tiles["y%d" % g, j] = y_sb
+
+        def scale(j):
+            if not in_range(j):
+                return
+            shift = work.tile([P, HEAD_DIM], F32, name="shift", tag="shift")
+            nc.scalar.activation(
+                out=shift[:],
+                in_=tiles["v", j][:],
+                func=ACT.Copy,
+                scale=tiles["neg_c", j][:, POOL_HEAD : POOL_HEAD + 1],
+            )
+            tiles["shift", j] = shift
+
+        def add(j):
+            if not in_range(j):
+                return
+            g = POOL_HEAD
+            y_sb = work.tile([P, HEAD_DIM], BF16, name="y_sb", tag="y_sb%d" % g)
+            nc.gpsimd.tensor_tensor(
+                out=y_sb[:], in0=tiles["a", j][:, g, :], in1=tiles["shift", j][:], op=ALU.add
+            )
+            tiles["y%d" % g, j] = y_sb
 
         def transpose(j, g):
-            if g == 0:
+            if not in_range(j):
+                return
+            if g == VECTOR_HEAD:
                 tiles["grouped", j] = work.tile(
                     [P, GROUP, PACK * HEAD_PASSES * P], BF16, name="grouped", tag="grouped", align_bytes=64
                 )
-            y_words = tiles["y", j][:, g, :].bitcast(F32)
+            y_words = tiles["y%d" % g, j][:].bitcast(F32)
             turned = psum_t.tile([P, HALVES, HEAD_PASSES * P], F32, name="turned", tag="turned%d" % g)
             pass_words = K_PASS // PAIR
             for c in range(HEAD_PASSES):
@@ -222,30 +261,36 @@ def tile_block_pb_k_kernel(tc, attn_out, v, x, wo_words, wo_scales, attn_scale, 
                 )
             for b in range(N_BANKS):
                 cols = slice(b * N_BANK, (b + 1) * N_BANK)
-                nc.vector.tensor_tensor(
+                nc.gpsimd.tensor_tensor(
                     out=result[:, cols], in0=scaled[:, cols], in1=tiles["x", i][:, cols], op=ALU.add
                 )
-            nc.sync.dma_start(out=out[0, i * P : (i + 1) * P, :], in_=result[:])
+                nc.sync.dma_start(out=out[0, i * P : (i + 1) * P, cols], in_=result[:, cols])
 
         for j in range(LOOKAHEAD):
             load(j)
         nc.sync.dma_start(out=gain[:], in_=attn_scale.partition_broadcast(P))
         square_sum(0)
         square_sum(1)
+        mirror(0)
         clamp(0)
         invert(0)
 
-        for s in range(UNITS + 2):
+        for s in range(UNITS + 4):
             load(s + LOOKAHEAD)
+            if s < KV_HEADS:
+                load_weights(s)
+            scale(s - 1)
+            add(s - 1)
+            transpose(s - 2, POOL_HEAD)
+            transpose(s - 1, VECTOR_HEAD)
+            mirror(s + 1)
+            square_sum(s + 2)
+            multiply(s - 3)
             if in_range(s):
-                dot(s, 0)
+                dot(s, VECTOR_HEAD)
                 clamp(s + 1)
-                dot(s, 1)
+                dot(s, POOL_HEAD)
                 invert(s + 1)
-                for g in range(GROUP):
-                    subtract(s, g)
-                    transpose(s, g)
-                square_sum(s + 2)
-            quantise(s - 1)
-            multiply(s - 1)
-            finish(s - 2)
+                subtract(s)
+            quantise(s - 2)
+            finish(s - 4)

@@ -35,7 +35,7 @@ LIVE_ROWS = 4
 
 TOKEN_TILES = TOKENS // P
 UNITS = TOKEN_TILES * KV_HEADS
-LOOKAHEAD = 3
+LOOKAHEAD = 4
 VECTOR_HEAD = 0
 POOL_HEAD = 1
 
@@ -97,7 +97,7 @@ def tile_block_pb_k_kernel(tc, attn_out, v, x, wo_words, wo_scales, attn_scale, 
             tiles["v", j] = v_sb
             tiles["a", j] = a_sb
             if h == KV_HEADS - 1:
-                x_sb = work.tile([P, D_OUT], BF16, name="x_sb", tag="x_sb")
+                x_sb = work.tile([P, D_OUT], BF16, name="x_sb", tag="x_sb", bufs=3)
                 nc.sync.dma_start(out=x_sb[:], in_=x[0, tokens, :])
                 tiles["x", i] = x_sb
 
@@ -144,7 +144,7 @@ def tile_block_pb_k_kernel(tc, attn_out, v, x, wo_words, wo_scales, attn_scale, 
             tiles["neg_inv", j] = neg_inv
 
         def dot(j, g):
-            if g == VECTOR_HEAD:
+            if g == POOL_HEAD:
                 tiles["neg_c", j] = small.tile([P, GROUP], F32, name="neg_c", tag="neg_c")
             products = work.tile([P, HEAD_DIM], BF16, name="products", tag="products")
             nc.vector.scalar_tensor_tensor(
@@ -186,7 +186,7 @@ def tile_block_pb_k_kernel(tc, attn_out, v, x, wo_words, wo_scales, attn_scale, 
             if not in_range(j):
                 return
             g = POOL_HEAD
-            y_sb = work.tile([P, HEAD_DIM], BF16, name="y_sb", tag="y_sb%d" % g)
+            y_sb = work.tile([P, HEAD_DIM], BF16, name="y_sb", tag="y_sb%d" % g, bufs=3)
             nc.gpsimd.tensor_tensor(
                 out=y_sb[:], in0=tiles["a", j][:, g, :], in1=tiles["shift", j][:], op=ALU.add
             )
@@ -197,7 +197,7 @@ def tile_block_pb_k_kernel(tc, attn_out, v, x, wo_words, wo_scales, attn_scale, 
                 return
             if g == VECTOR_HEAD:
                 tiles["grouped", j] = work.tile(
-                    [P, GROUP, PACK * HEAD_PASSES * P], BF16, name="grouped", tag="grouped", align_bytes=64
+                    [P, GROUP, PACK * HEAD_PASSES * P], BF16, name="grouped", tag="grouped", bufs=4, align_bytes=64
                 )
             y_words = tiles["y%d" % g, j][:].bitcast(F32)
             turned = psum_t.tile([P, HALVES, HEAD_PASSES * P], F32, name="turned", tag="turned%d" % g)
@@ -234,10 +234,10 @@ def tile_block_pb_k_kernel(tc, attn_out, v, x, wo_words, wo_scales, attn_scale, 
             if h == 0:
                 for b in range(N_BANKS):
                     tiles["acc%d" % b, i] = psum_acc.tile([P, N_BANK], F32, name="acc", tag="acc%d" % b)
-            for c in range(UNIT_PASSES):
-                w_pass = h * UNIT_PASSES + c
-                token_cols = slice(c * P, (c + 1) * P)
-                for b in range(N_BANKS):
+            for b in range(N_BANKS):
+                for c in range(UNIT_PASSES):
+                    w_pass = h * UNIT_PASSES + c
+                    token_cols = slice(c * P, (c + 1) * P)
                     nc.tensor.matmul_mx(
                         out=tiles["acc%d" % b, i][:],
                         lhsT=tiles["y_codes", j][:, token_cols].bitcast(FP8X4),
@@ -271,26 +271,28 @@ def tile_block_pb_k_kernel(tc, attn_out, v, x, wo_words, wo_scales, attn_scale, 
         nc.sync.dma_start(out=gain[:], in_=attn_scale.partition_broadcast(P))
         square_sum(0)
         square_sum(1)
+        square_sum(2)
         mirror(0)
         clamp(0)
         invert(0)
 
-        for s in range(UNITS + 4):
+        for s in range(UNITS + 6):
             load(s + LOOKAHEAD)
             if s < KV_HEADS:
                 load_weights(s)
             scale(s - 1)
             add(s - 1)
-            transpose(s - 2, POOL_HEAD)
+            transpose(s - 3, POOL_HEAD)
             transpose(s - 1, VECTOR_HEAD)
             mirror(s + 1)
-            square_sum(s + 2)
-            multiply(s - 3)
+            square_sum(s + 3)
+            multiply(s - 5)
             if in_range(s):
-                dot(s, VECTOR_HEAD)
-                clamp(s + 1)
                 dot(s, POOL_HEAD)
+                clamp(s + 1)
+                dot(s, VECTOR_HEAD)
+            quantise(s - 4)
+            if in_range(s):
                 invert(s + 1)
                 subtract(s)
-            quantise(s - 2)
-            finish(s - 4)
+            finish(s - 6)

@@ -38,6 +38,7 @@ UNITS = TOKEN_TILES * KV_HEADS
 LOOKAHEAD = 4
 VECTOR_HEAD = 0
 POOL_HEAD = 1
+POOL_PIECE = 256
 
 FLOPS = 2 * TOKENS * KV_HEADS * GROUP * HEAD_DIM * D_OUT
 
@@ -187,9 +188,11 @@ def tile_block_pb_k_kernel(tc, attn_out, v, x, wo_words, wo_scales, attn_scale, 
                 return
             g = POOL_HEAD
             y_sb = work.tile([P, HEAD_DIM], BF16, name="y_sb", tag="y_sb%d" % g, bufs=3)
-            nc.gpsimd.tensor_tensor(
-                out=y_sb[:], in0=tiles["a", j][:, g, :], in1=tiles["shift", j][:], op=ALU.add
-            )
+            for first in range(0, HEAD_DIM, POOL_PIECE):
+                cols = slice(first, first + POOL_PIECE)
+                nc.gpsimd.tensor_tensor(
+                    out=y_sb[:, cols], in0=tiles["a", j][:, g, cols], in1=tiles["shift", j][:, cols], op=ALU.add
+                )
             tiles["y%d" % g, j] = y_sb
 
         def transpose(j, g):
@@ -260,10 +263,12 @@ def tile_block_pb_k_kernel(tc, attn_out, v, x, wo_words, wo_scales, attn_scale, 
                     out=scaled[:, cols], in0=tiles["acc%d" % b, i][:], in1=gain[:, cols], op=ALU.mult
                 )
             for b in range(N_BANKS):
+                for first in range(b * N_BANK, (b + 1) * N_BANK, POOL_PIECE):
+                    cols = slice(first, first + POOL_PIECE)
+                    nc.gpsimd.tensor_tensor(
+                        out=result[:, cols], in0=scaled[:, cols], in1=tiles["x", i][:, cols], op=ALU.add
+                    )
                 cols = slice(b * N_BANK, (b + 1) * N_BANK)
-                nc.gpsimd.tensor_tensor(
-                    out=result[:, cols], in0=scaled[:, cols], in1=tiles["x", i][:, cols], op=ALU.add
-                )
                 nc.sync.dma_start(out=out[0, i * P : (i + 1) * P, cols], in_=result[:, cols])
 
         for j in range(LOOKAHEAD):
@@ -289,8 +294,8 @@ def tile_block_pb_k_kernel(tc, attn_out, v, x, wo_words, wo_scales, attn_scale, 
             multiply(s - 5)
             if in_range(s):
                 dot(s, POOL_HEAD)
-                clamp(s + 1)
                 dot(s, VECTOR_HEAD)
+                clamp(s + 1)
             quantise(s - 4)
             if in_range(s):
                 invert(s + 1)

@@ -35,10 +35,9 @@ LIVE_ROWS = 4
 
 TOKEN_TILES = TOKENS // P
 UNITS = TOKEN_TILES * KV_HEADS
-LOOKAHEAD = 4
+LOOKAHEAD = 3
 VECTOR_HEAD = 0
 POOL_HEAD = 1
-POOL_PIECE = 256
 
 FLOPS = 2 * TOKENS * KV_HEADS * GROUP * HEAD_DIM * D_OUT
 
@@ -98,7 +97,7 @@ def tile_block_pb_k_kernel(tc, attn_out, v, x, wo_words, wo_scales, attn_scale, 
             tiles["v", j] = v_sb
             tiles["a", j] = a_sb
             if h == KV_HEADS - 1:
-                x_sb = work.tile([P, D_OUT], BF16, name="x_sb", tag="x_sb", bufs=3)
+                x_sb = work.tile([P, D_OUT], BF16, name="x_sb", tag="x_sb")
                 nc.sync.dma_start(out=x_sb[:], in_=x[0, tokens, :])
                 tiles["x", i] = x_sb
 
@@ -187,21 +186,15 @@ def tile_block_pb_k_kernel(tc, attn_out, v, x, wo_words, wo_scales, attn_scale, 
             if not in_range(j):
                 return
             g = POOL_HEAD
-            y_sb = work.tile([P, HEAD_DIM], BF16, name="y_sb", tag="y_sb%d" % g, bufs=3)
-            for first in range(0, HEAD_DIM, POOL_PIECE):
-                cols = slice(first, first + POOL_PIECE)
-                nc.gpsimd.tensor_tensor(
-                    out=y_sb[:, cols], in0=tiles["a", j][:, g, cols], in1=tiles["shift", j][:, cols], op=ALU.add
-                )
+            y_sb = work.tile([P, HEAD_DIM], BF16, name="y_sb", tag="y_sb%d" % g)
+            nc.gpsimd.tensor_tensor(
+                out=y_sb[:], in0=tiles["a", j][:, g, :], in1=tiles["shift", j][:], op=ALU.add
+            )
             tiles["y%d" % g, j] = y_sb
 
-        def transpose(j, g):
+        def turn(j, g):
             if not in_range(j):
                 return
-            if g == VECTOR_HEAD:
-                tiles["grouped", j] = work.tile(
-                    [P, GROUP, PACK * HEAD_PASSES * P], BF16, name="grouped", tag="grouped", bufs=4, align_bytes=64
-                )
             y_words = tiles["y%d" % g, j][:].bitcast(F32)
             turned = psum_t.tile([P, HALVES, HEAD_PASSES * P], F32, name="turned", tag="turned%d" % g)
             pass_words = K_PASS // PAIR
@@ -212,9 +205,18 @@ def tile_block_pb_k_kernel(tc, attn_out, v, x, wo_words, wo_scales, attn_scale, 
                         y_words[:, c * pass_words + u : (c + 1) * pass_words : HALVES],
                         identity[:],
                     )
+            tiles["turned%d" % g, j] = turned
+
+        def regroup(j, g):
+            if not in_range(j):
+                return
+            if g == VECTOR_HEAD:
+                tiles["grouped", j] = work.tile(
+                    [P, GROUP, PACK * HEAD_PASSES * P], BF16, name="grouped", tag="grouped", align_bytes=64
+                )
             nc.scalar.copy(
                 out=tiles["grouped", j][:, g, :].bitcast(F32).rearrange("p (q u) -> p q u", u=HALVES),
-                in_=turned[:].rearrange("p u q -> p q u"),
+                in_=tiles["turned%d" % g, j][:].rearrange("p u q -> p q u"),
             )
 
         def quantise(j):
@@ -263,41 +265,41 @@ def tile_block_pb_k_kernel(tc, attn_out, v, x, wo_words, wo_scales, attn_scale, 
                     out=scaled[:, cols], in0=tiles["acc%d" % b, i][:], in1=gain[:, cols], op=ALU.mult
                 )
             for b in range(N_BANKS):
-                for first in range(b * N_BANK, (b + 1) * N_BANK, POOL_PIECE):
-                    cols = slice(first, first + POOL_PIECE)
-                    nc.gpsimd.tensor_tensor(
-                        out=result[:, cols], in0=scaled[:, cols], in1=tiles["x", i][:, cols], op=ALU.add
-                    )
                 cols = slice(b * N_BANK, (b + 1) * N_BANK)
+                nc.vector.tensor_tensor(
+                    out=result[:, cols], in0=scaled[:, cols], in1=tiles["x", i][:, cols], op=ALU.add
+                )
                 nc.sync.dma_start(out=out[0, i * P : (i + 1) * P, cols], in_=result[:, cols])
 
         for j in range(LOOKAHEAD):
             load(j)
-        nc.sync.dma_start(out=gain[:], in_=attn_scale.partition_broadcast(P))
         square_sum(0)
         square_sum(1)
-        square_sum(2)
         mirror(0)
         clamp(0)
         invert(0)
 
-        for s in range(UNITS + 6):
+        for s in range(UNITS + 3):
             load(s + LOOKAHEAD)
             if s < KV_HEADS:
                 load_weights(s)
-            scale(s - 1)
-            add(s - 1)
-            transpose(s - 3, POOL_HEAD)
-            transpose(s - 1, VECTOR_HEAD)
+            elif s == KV_HEADS:
+                nc.sync.dma_start(out=gain[:], in_=attn_scale.partition_broadcast(P))
+            turn(s - 1, VECTOR_HEAD)
+            turn(s - 1, POOL_HEAD)
             mirror(s + 1)
-            square_sum(s + 3)
-            multiply(s - 5)
             if in_range(s):
                 dot(s, POOL_HEAD)
-                dot(s, VECTOR_HEAD)
-                clamp(s + 1)
-            quantise(s - 4)
+            scale(s)
+            add(s)
+            clamp(s + 1)
+            quantise(s - 2)
+            multiply(s - 2)
             if in_range(s):
+                dot(s, VECTOR_HEAD)
                 invert(s + 1)
                 subtract(s)
-            finish(s - 6)
+            regroup(s - 1, VECTOR_HEAD)
+            regroup(s - 1, POOL_HEAD)
+            square_sum(s + 2)
+            finish(s - 3)

@@ -36,8 +36,10 @@ LIVE_ROWS = 4
 TOKEN_TILES = TOKENS // P
 UNITS = TOKEN_TILES * KV_HEADS
 LOOKAHEAD = 3
-VECTOR_HEAD = 0
+SHARED_HEAD = 0
 POOL_HEAD = 1
+PERMUTE = True
+HALF = HEAD_DIM // 2
 
 FLOPS = 2 * TOKENS * KV_HEADS * GROUP * HEAD_DIM * D_OUT
 
@@ -48,10 +50,13 @@ def tile_block_pb_k_kernel(tc, attn_out, v, x, wo_words, wo_scales, attn_scale, 
         consts = ctx.enter_context(tc.tile_pool(name="consts", bufs=1))
         inputs = ctx.enter_context(tc.tile_pool(name="inputs", bufs=LOOKAHEAD + 2))
         work = ctx.enter_context(tc.tile_pool(name="work", bufs=2))
+        deep = ctx.enter_context(tc.tile_pool(name="deep", bufs=3))
+        codes = ctx.enter_context(tc.tile_pool(name="codes", bufs=4))
         small = ctx.enter_context(tc.tile_pool(name="small", bufs=4))
         psum_v = ctx.enter_context(tc.psum_pool(name="psum_v", bufs=2))
         psum_t = ctx.enter_context(tc.psum_pool(name="psum_t", bufs=1))
-        psum_acc = ctx.enter_context(tc.psum_pool(name="psum_acc", bufs=2))
+        psum_acc = ctx.enter_context(tc.psum_pool(name="psum_acc", bufs=3))
+        psum_x = ctx.enter_context(tc.psum_pool(name="psum_x", bufs=1))
         ctx.enter_context(tc.manual_schedule())
 
         tiles = {}
@@ -68,6 +73,14 @@ def tile_block_pb_k_kernel(tc, attn_out, v, x, wo_words, wo_scales, attn_scale, 
 
         def in_range(j):
             return 0 <= j < UNITS
+
+        def by_half(ap):
+            if PERMUTE:
+                return ap.rearrange("p (q u e) -> p u q e", u=HALVES, e=PAIR)
+            return ap.rearrange("p (u q e) -> p u q e", u=HALVES, e=PAIR)
+
+        def laid(ap):
+            return ap.rearrange("p (u q e) -> p u q e", u=HALVES, e=PAIR)
 
         def load_weights(h):
             passes = slice(h * UNIT_PASSES, (h + 1) * UNIT_PASSES)
@@ -122,6 +135,17 @@ def tile_block_pb_k_kernel(tc, attn_out, v, x, wo_words, wo_scales, attn_scale, 
                 )
             tiles["v_ps", j] = v_ps
 
+        def mirror_x(i):
+            if not 0 <= i < TOKEN_TILES:
+                return
+            x_ps = psum_x.tile([P, D_OUT], BF16, name="x_ps", tag="x_ps")
+            for b in range(N_BANKS):
+                cols = slice(b * N_BANK, (b + 1) * N_BANK)
+                nc.tensor.matmul(
+                    out=x_ps[:, cols], lhsT=identity_bf[:], rhs=tiles["x", i][:, cols], start=True, stop=True
+                )
+            tiles["x_ps", i] = x_ps
+
         def clamp(j):
             if not in_range(j):
                 return
@@ -144,8 +168,10 @@ def tile_block_pb_k_kernel(tc, attn_out, v, x, wo_words, wo_scales, attn_scale, 
             tiles["neg_inv", j] = neg_inv
 
         def dot(j, g):
-            if g == POOL_HEAD:
-                tiles["neg_c", j] = small.tile([P, GROUP], F32, name="neg_c", tag="neg_c")
+            if not in_range(j):
+                return
+            neg_c = small.tile([P, 1], F32, name="neg_c", tag="neg_c%d" % g)
+            tiles["neg_c%d" % g, j] = neg_c
             products = work.tile([P, HEAD_DIM], BF16, name="products", tag="products")
             nc.vector.scalar_tensor_tensor(
                 out=products[:],
@@ -154,43 +180,61 @@ def tile_block_pb_k_kernel(tc, attn_out, v, x, wo_words, wo_scales, attn_scale, 
                 in1=tiles["v_ps", j][:],
                 op0=ALU.mult,
                 op1=ALU.mult,
-                accum_out=tiles["neg_c", j][:, g : g + 1],
+                accum_out=neg_c[:],
             )
 
-        def subtract(j):
-            g = VECTOR_HEAD
-            y_sb = work.tile([P, HEAD_DIM], BF16, name="y_sb", tag="y_sb%d" % g)
+        def new_y(j, g):
+            tiles["y%d" % g, j] = deep.tile([P, HEAD_DIM], BF16, name="y_sb", tag="y_sb%d" % g)
+
+        def subtract(j, g, u):
+            if not in_range(j):
+                return
             nc.vector.scalar_tensor_tensor(
-                out=y_sb[:],
-                in0=tiles["v_ps", j][:],
-                scalar=tiles["neg_c", j][:, g : g + 1],
-                in1=tiles["a", j][:, g, :],
+                out=laid(tiles["y%d" % g, j][:])[:, u],
+                in0=by_half(tiles["v_ps", j][:])[:, u],
+                scalar=tiles["neg_c%d" % g, j][:, 0:1],
+                in1=by_half(tiles["a", j][:, g, :])[:, u],
                 op0=ALU.mult,
                 op1=ALU.add,
             )
-            tiles["y%d" % g, j] = y_sb
 
-        def scale(j):
+        def scale(j, g):
             if not in_range(j):
                 return
-            shift = work.tile([P, HEAD_DIM], F32, name="shift", tag="shift")
-            nc.scalar.activation(
-                out=shift[:],
-                in_=tiles["v", j][:],
-                func=ACT.Copy,
-                scale=tiles["neg_c", j][:, POOL_HEAD : POOL_HEAD + 1],
-            )
-            tiles["shift", j] = shift
+            if g == POOL_HEAD:
+                shift = work.tile([P, HEAD_DIM], F32, name="shift", tag="shift%d" % g)
+                nc.scalar.activation(
+                    out=laid(shift[:]), in_=by_half(tiles["v", j][:]), func=ACT.Copy, scale=tiles["neg_c%d" % g, j][:, 0:1]
+                )
+            else:
+                shift = work.tile([P, HALF], F32, name="shift", tag="shift%d" % g)
+                nc.scalar.activation(
+                    out=shift[:].rearrange("p (q e) -> p q e", e=PAIR),
+                    in_=by_half(tiles["v", j][:])[:, 1],
+                    func=ACT.Copy,
+                    scale=tiles["neg_c%d" % g, j][:, 0:1],
+                )
+            tiles["shift%d" % g, j] = shift
 
-        def add(j):
+        def add(j, g):
             if not in_range(j):
                 return
-            g = POOL_HEAD
-            y_sb = work.tile([P, HEAD_DIM], BF16, name="y_sb", tag="y_sb%d" % g)
-            nc.gpsimd.tensor_tensor(
-                out=y_sb[:], in0=tiles["a", j][:, g, :], in1=tiles["shift", j][:], op=ALU.add
-            )
-            tiles["y%d" % g, j] = y_sb
+            if g == POOL_HEAD:
+                new_y(j, g)
+                nc.gpsimd.tensor_tensor(
+                    out=laid(tiles["y%d" % g, j][:]),
+                    in0=by_half(tiles["a", j][:, g, :]),
+                    in1=laid(tiles["shift%d" % g, j][:]),
+                    op=ALU.add,
+                )
+            else:
+                new_y(j, g)
+                nc.gpsimd.tensor_tensor(
+                    out=laid(tiles["y%d" % g, j][:])[:, 1],
+                    in0=by_half(tiles["a", j][:, g, :])[:, 1],
+                    in1=tiles["shift%d" % g, j][:].rearrange("p (q e) -> p q e", e=PAIR),
+                    op=ALU.add,
+                )
 
         def turn(j, g):
             if not in_range(j):
@@ -198,19 +242,20 @@ def tile_block_pb_k_kernel(tc, attn_out, v, x, wo_words, wo_scales, attn_scale, 
             y_words = tiles["y%d" % g, j][:].bitcast(F32)
             turned = psum_t.tile([P, HALVES, HEAD_PASSES * P], F32, name="turned", tag="turned%d" % g)
             pass_words = K_PASS // PAIR
-            for c in range(HEAD_PASSES):
-                for u in range(HALVES):
-                    nc.tensor.transpose(
-                        turned[:, u, c * P : (c + 1) * P],
-                        y_words[:, c * pass_words + u : (c + 1) * pass_words : HALVES],
-                        identity[:],
-                    )
+            for u in range(HALVES):
+                for c in range(HEAD_PASSES):
+                    if PERMUTE:
+                        first = u * (HEAD_PASSES * P) + c * P
+                        words = y_words[:, first : first + P]
+                    else:
+                        words = y_words[:, c * pass_words + u : (c + 1) * pass_words : HALVES]
+                    nc.tensor.transpose(turned[:, u, c * P : (c + 1) * P], words, identity[:])
             tiles["turned%d" % g, j] = turned
 
-        def regroup(j, g):
+        def regroup(j, g, first):
             if not in_range(j):
                 return
-            if g == VECTOR_HEAD:
+            if first:
                 tiles["grouped", j] = work.tile(
                     [P, GROUP, PACK * HEAD_PASSES * P], BF16, name="grouped", tag="grouped", align_bytes=64
                 )
@@ -219,28 +264,30 @@ def tile_block_pb_k_kernel(tc, attn_out, v, x, wo_words, wo_scales, attn_scale, 
                 in_=tiles["turned%d" % g, j][:].rearrange("p u q -> p q u"),
             )
 
-        def quantise(j):
+        def quantise(j, heads):
             if not in_range(j):
                 return
-            y_codes = work.tile([P, UNIT_PASSES * P], U32, name="y_codes", tag="y_codes", align_bytes=64)
-            y_planes = work.tile([P, UNIT_PASSES * P], U8, name="y_planes", tag="y_planes", align_bytes=64)
+            if ("y_codes", j) not in tiles:
+                tiles["y_codes", j] = codes.tile([P, UNIT_PASSES * P], U32, name="y_codes", tag="y_codes", align_bytes=64)
+                tiles["y_planes", j] = codes.tile([P, UNIT_PASSES * P], U8, name="y_planes", tag="y_planes", align_bytes=64)
+            first = min(heads) * HEAD_PASSES * P
+            width = len(heads) * HEAD_PASSES * P
             nc.vector.quantize_mx(
-                out=y_codes[:].bitcast(FP8X4),
-                scales=y_planes[:],
-                in_=tiles["grouped", j][:].rearrange("p g c -> p (g c)"),
+                out=tiles["y_codes", j][:, first : first + width].bitcast(FP8X4),
+                scales=tiles["y_planes", j][:, first : first + width],
+                in_=tiles["grouped", j][:].rearrange("p g c -> p (g c)")[:, PACK * first : PACK * (first + width)],
             )
-            tiles["y_codes", j] = y_codes
-            tiles["y_planes", j] = y_planes
 
-        def multiply(j):
+        def multiply(j, heads, opens, closes):
             if not in_range(j):
                 return
             i, h = divmod(j, KV_HEADS)
-            if h == 0:
+            if h == 0 and opens:
                 for b in range(N_BANKS):
-                    tiles["acc%d" % b, i] = psum_acc.tile([P, N_BANK], F32, name="acc", tag="acc%d" % b)
+                    tiles["acc%d" % b, i] = psum_acc.tile([P, N_BANK], F32, name="acc", tag="acc")
+            unit_passes = [g * HEAD_PASSES + c for g in heads for c in range(HEAD_PASSES)]
             for b in range(N_BANKS):
-                for c in range(UNIT_PASSES):
+                for c in unit_passes:
                     w_pass = h * UNIT_PASSES + c
                     token_cols = slice(c * P, (c + 1) * P)
                     nc.tensor.matmul_mx(
@@ -249,57 +296,85 @@ def tile_block_pb_k_kernel(tc, attn_out, v, x, wo_words, wo_scales, attn_scale, 
                         lhsT_scale=tiles["y_planes", j][:, token_cols],
                         rhs=w_words[:, w_pass, b * PAIR * N_BANK : (b + 1) * PAIR * N_BANK].bitcast(FP4X4),
                         rhs_scale=w_planes[:, w_pass, b * N_BANK : (b + 1) * N_BANK],
-                        start=(w_pass == 0),
-                        stop=(w_pass == PASSES - 1),
+                        start=(h == 0 and opens and c == unit_passes[0]),
+                        stop=(h == KV_HEADS - 1 and closes and c == unit_passes[-1]),
                     )
 
-        def finish(j):
-            i, h = divmod(j, KV_HEADS)
-            if not in_range(j) or h != KV_HEADS - 1:
+        def finish_piece(i, piece):
+            if not 0 <= i < TOKEN_TILES:
                 return
-            scaled = work.tile([P, D_OUT], F32, name="scaled", tag="scaled")
-            result = work.tile([P, D_OUT], F32, name="result", tag="result")
-            for b in range(N_BANKS):
-                cols = slice(b * N_BANK, (b + 1) * N_BANK)
+            b = piece % N_BANKS
+            cols = slice(b * N_BANK, (b + 1) * N_BANK)
+            if piece == 0:
+                tiles["scaled", i] = work.tile([P, D_OUT], F32, name="scaled", tag="scaled")
+                tiles["result", i] = work.tile([P, D_OUT], F32, name="result", tag="result")
+            if piece < N_BANKS:
                 nc.vector.tensor_tensor(
-                    out=scaled[:, cols], in0=tiles["acc%d" % b, i][:], in1=gain[:, cols], op=ALU.mult
+                    out=tiles["scaled", i][:, cols], in0=tiles["acc%d" % b, i][:], in1=gain[:, cols], op=ALU.mult
                 )
-            for b in range(N_BANKS):
-                cols = slice(b * N_BANK, (b + 1) * N_BANK)
+            else:
                 nc.vector.tensor_tensor(
-                    out=result[:, cols], in0=scaled[:, cols], in1=tiles["x", i][:, cols], op=ALU.add
+                    out=tiles["result", i][:, cols], in0=tiles["scaled", i][:, cols], in1=tiles["x_ps", i][:, cols], op=ALU.add
                 )
-                nc.sync.dma_start(out=out[0, i * P : (i + 1) * P, cols], in_=result[:, cols])
+                nc.sync.dma_start(out=out[0, i * P : (i + 1) * P, cols], in_=tiles["result", i][:, cols])
 
         for j in range(LOOKAHEAD):
             load(j)
         square_sum(0)
-        square_sum(1)
         mirror(0)
         clamp(0)
         invert(0)
+        square_sum(1)
+        clamp(1)
 
-        for s in range(UNITS + 3):
+        BOTH = (SHARED_HEAD, POOL_HEAD)
+        LAST = UNITS - 1
+        for s in range(UNITS):
             load(s + LOOKAHEAD)
             if s < KV_HEADS:
                 load_weights(s)
             elif s == KV_HEADS:
                 nc.sync.dma_start(out=gain[:], in_=attn_scale.partition_broadcast(P))
-            turn(s - 1, VECTOR_HEAD)
-            turn(s - 1, POOL_HEAD)
-            mirror(s + 1)
-            if in_range(s):
-                dot(s, POOL_HEAD)
-            scale(s)
-            add(s)
-            clamp(s + 1)
-            quantise(s - 2)
-            multiply(s - 2)
-            if in_range(s):
-                dot(s, VECTOR_HEAD)
-                invert(s + 1)
-                subtract(s)
-            regroup(s - 1, VECTOR_HEAD)
-            regroup(s - 1, POOL_HEAD)
+            done, piece = divmod(s - 2 - KV_HEADS, KV_HEADS)
+            dot(s, POOL_HEAD)
+            invert(s + 1)
+            if s < LAST:
+                scale(s, POOL_HEAD)
+            if piece == 1:
+                mirror_x(done)
+            finish_piece(done, piece)
             square_sum(s + 2)
-            finish(s - 3)
+            subtract(s - 1, SHARED_HEAD, 0)
+            turn(s - 1, SHARED_HEAD)
+            mirror(s + 1)
+            dot(s, SHARED_HEAD)
+            scale(s, SHARED_HEAD)
+            add(s, SHARED_HEAD)
+            if s < LAST:
+                add(s, POOL_HEAD)
+            quantise(s - 2, BOTH)
+            clamp(s + 2)
+            turn(s - 1, POOL_HEAD)
+            multiply(s - 2, BOTH, True, True)
+            regroup(s - 1, POOL_HEAD, True)
+            regroup(s - 1, SHARED_HEAD, False)
+
+        new_y(LAST, POOL_HEAD)
+        subtract(LAST, POOL_HEAD, 0)
+        subtract(LAST, POOL_HEAD, 1)
+        turn(LAST, POOL_HEAD)
+        regroup(LAST, POOL_HEAD, True)
+        subtract(LAST, SHARED_HEAD, 0)
+        quantise(LAST - 1, BOTH)
+        turn(LAST, SHARED_HEAD)
+        regroup(LAST, SHARED_HEAD, False)
+        multiply(LAST - 1, BOTH, True, True)
+        finish_piece(TOKEN_TILES - 2, 2)
+        finish_piece(TOKEN_TILES - 2, 3)
+        mirror_x(TOKEN_TILES - 1)
+        quantise(LAST, (POOL_HEAD,))
+        multiply(LAST, (POOL_HEAD,), True, False)
+        quantise(LAST, (SHARED_HEAD,))
+        multiply(LAST, (SHARED_HEAD,), False, True)
+        for piece in (0, 2, 1, 3):
+            finish_piece(TOKEN_TILES - 1, piece)

@@ -35,7 +35,7 @@ LIVE_ROWS = 4
 
 TOKEN_TILES = TOKENS // P
 UNITS = TOKEN_TILES * KV_HEADS
-LOOKAHEAD = 3
+LOOKAHEAD = 4
 SHARED_HEAD = 0
 POOL_HEAD = 1
 PERMUTE = True
@@ -109,10 +109,13 @@ def tile_block_pb_k_kernel(tc, attn_out, v, x, wo_words, wo_scales, attn_scale, 
             )
             tiles["v", j] = v_sb
             tiles["a", j] = a_sb
-            if h == KV_HEADS - 1:
-                x_sb = work.tile([P, D_OUT], BF16, name="x_sb", tag="x_sb")
-                nc.sync.dma_start(out=x_sb[:], in_=x[0, tokens, :])
-                tiles["x", i] = x_sb
+
+        def load_x(i):
+            if not 0 <= i < TOKEN_TILES:
+                return
+            x_sb = work.tile([P, D_OUT], BF16, name="x_sb", tag="x_sb")
+            nc.sync.dma_start(out=x_sb[:], in_=x[0, i * P : (i + 1) * P, :])
+            tiles["x", i] = x_sb
 
         def square_sum(j):
             if not in_range(j):
@@ -278,15 +281,15 @@ def tile_block_pb_k_kernel(tc, attn_out, v, x, wo_words, wo_scales, attn_scale, 
                 in_=tiles["grouped", j][:].rearrange("p g c -> p (g c)")[:, PACK * first : PACK * (first + width)],
             )
 
-        def multiply(j, heads, opens, closes):
+        def multiply(j, heads, opens, closes, banks=(0, 1)):
             if not in_range(j):
                 return
             i, h = divmod(j, KV_HEADS)
-            if h == 0 and opens:
+            if h == 0 and opens and banks[0] == 0:
                 for b in range(N_BANKS):
                     tiles["acc%d" % b, i] = psum_acc.tile([P, N_BANK], F32, name="acc", tag="acc")
             unit_passes = [g * HEAD_PASSES + c for g in heads for c in range(HEAD_PASSES)]
-            for b in range(N_BANKS):
+            for b in banks:
                 for c in unit_passes:
                     w_pass = h * UNIT_PASSES + c
                     token_cols = slice(c * P, (c + 1) * P)
@@ -314,7 +317,7 @@ def tile_block_pb_k_kernel(tc, attn_out, v, x, wo_words, wo_scales, attn_scale, 
                 )
             else:
                 nc.vector.tensor_tensor(
-                    out=tiles["result", i][:, cols], in0=tiles["scaled", i][:, cols], in1=tiles["x_ps", i][:, cols], op=ALU.add
+                    out=tiles["result", i][:, cols], in0=tiles["scaled", i][:, cols], in1=tiles.get(("x_ps", i), tiles["x", i])[:, cols], op=ALU.add
                 )
                 nc.sync.dma_start(out=out[0, i * P : (i + 1) * P, cols], in_=tiles["result", i][:, cols])
 
@@ -325,7 +328,8 @@ def tile_block_pb_k_kernel(tc, attn_out, v, x, wo_words, wo_scales, attn_scale, 
         clamp(0)
         invert(0)
         square_sum(1)
-        clamp(1)
+        mirror(1)
+        square_sum(2)
 
         BOTH = (SHARED_HEAD, POOL_HEAD)
         LAST = UNITS - 1
@@ -335,29 +339,41 @@ def tile_block_pb_k_kernel(tc, attn_out, v, x, wo_words, wo_scales, attn_scale, 
                 load_weights(s)
             elif s == KV_HEADS:
                 nc.sync.dma_start(out=gain[:], in_=attn_scale.partition_broadcast(P))
+            if s % KV_HEADS == 1:
+                load_x(s // KV_HEADS - 1)
+            if s == LAST:
+                load_x(TOKEN_TILES - 1)
             done, piece = divmod(s - 2 - KV_HEADS, KV_HEADS)
             dot(s, POOL_HEAD)
-            invert(s + 1)
             if s < LAST:
                 scale(s, POOL_HEAD)
-            if piece == 1:
-                mirror_x(done)
-            finish_piece(done, piece)
-            square_sum(s + 2)
-            subtract(s - 1, SHARED_HEAD, 0)
-            turn(s - 1, SHARED_HEAD)
-            mirror(s + 1)
             dot(s, SHARED_HEAD)
             scale(s, SHARED_HEAD)
             add(s, SHARED_HEAD)
             if s < LAST:
                 add(s, POOL_HEAD)
-            quantise(s - 2, BOTH)
+            if s == 0:
+                clamp(1)
+            invert(s + 1)
             clamp(s + 2)
-            turn(s - 1, POOL_HEAD)
-            multiply(s - 2, BOTH, True, True)
-            regroup(s - 1, POOL_HEAD, True)
-            regroup(s - 1, SHARED_HEAD, False)
+            quantise(s - 2, BOTH)
+            if piece == 1:
+                mirror_x(done)
+            finish_piece(done, piece)
+            regroup(s - 1, SHARED_HEAD, True)
+            square_sum(s + 3)
+            if s == LAST:
+                multiply(s - 2, BOTH, True, True, (0,))
+                turn(s - 1, POOL_HEAD)
+                multiply(s - 2, BOTH, True, True, (1,))
+            else:
+                turn(s - 1, POOL_HEAD)
+                multiply(s - 2, BOTH, True, True)
+            regroup(s - 1, POOL_HEAD, False)
+            if s < LAST:
+                subtract(s, SHARED_HEAD, 0)
+                mirror(s + 2)
+                turn(s, SHARED_HEAD)
 
         new_y(LAST, POOL_HEAD)
         subtract(LAST, POOL_HEAD, 0)
@@ -371,10 +387,9 @@ def tile_block_pb_k_kernel(tc, attn_out, v, x, wo_words, wo_scales, attn_scale, 
         multiply(LAST - 1, BOTH, True, True)
         finish_piece(TOKEN_TILES - 2, 2)
         finish_piece(TOKEN_TILES - 2, 3)
-        mirror_x(TOKEN_TILES - 1)
         quantise(LAST, (POOL_HEAD,))
         multiply(LAST, (POOL_HEAD,), True, False)
         quantise(LAST, (SHARED_HEAD,))
         multiply(LAST, (SHARED_HEAD,), False, True)
-        for piece in (0, 2, 1, 3):
+        for piece in range(4):
             finish_piece(TOKEN_TILES - 1, piece)

@@ -38,7 +38,9 @@ UNITS = TOKEN_TILES * KV_HEADS
 LOOKAHEAD = 4
 SHARED_HEAD = 0
 POOL_HEAD = 1
-PERMUTE = True
+HEAD_Q = HEAD_DIM // PACK
+UNIT_Q = GROUP * HEAD_Q
+VECTOR_Q = 128
 HALF = HEAD_DIM // 2
 
 FLOPS = 2 * TOKENS * KV_HEADS * GROUP * HEAD_DIM * D_OUT
@@ -75,9 +77,7 @@ def tile_block_pb_k_kernel(tc, attn_out, v, x, wo_words, wo_scales, attn_scale, 
             return 0 <= j < UNITS
 
         def by_half(ap):
-            if PERMUTE:
-                return ap.rearrange("p (q u e) -> p u q e", u=HALVES, e=PAIR)
-            return ap.rearrange("p (u q e) -> p u q e", u=HALVES, e=PAIR)
+            return ap.rearrange("p (q u e) -> p u q e", u=HALVES, e=PAIR)
 
         def laid(ap):
             return ap.rearrange("p (u q e) -> p u q e", u=HALVES, e=PAIR)
@@ -186,17 +186,24 @@ def tile_block_pb_k_kernel(tc, attn_out, v, x, wo_words, wo_scales, attn_scale, 
                 accum_out=neg_c[:],
             )
 
-        def new_y(j, g):
-            tiles["y%d" % g, j] = deep.tile([P, HEAD_DIM], BF16, name="y_sb", tag="y_sb%d" % g)
+        def new_y(j):
+            tiles["y_first", j] = deep.tile([P, PACK * VECTOR_Q], BF16, name="y_first", tag="y_first")
+            tiles["y_rest", j] = deep.tile([P, PACK * (UNIT_Q - VECTOR_Q)], BF16, name="y_rest", tag="y_rest")
 
-        def subtract(j, g, u):
+        def subtract(j, g, u, q_first, q_end):
             if not in_range(j):
                 return
+            unit_first = g * HEAD_Q + q_first
+            unit_end = g * HEAD_Q + q_end
+            if unit_end <= VECTOR_Q:
+                y_part = laid(tiles["y_first", j][:])[:, u, unit_first:unit_end, :]
+            else:
+                y_part = laid(tiles["y_rest", j][:])[:, u, unit_first - VECTOR_Q : unit_end - VECTOR_Q, :]
             nc.vector.scalar_tensor_tensor(
-                out=laid(tiles["y%d" % g, j][:])[:, u],
-                in0=by_half(tiles["v_ps", j][:])[:, u],
+                out=y_part,
+                in0=by_half(tiles["v_ps", j][:])[:, u, q_first:q_end, :],
                 scalar=tiles["neg_c%d" % g, j][:, 0:1],
-                in1=by_half(tiles["a", j][:, g, :])[:, u],
+                in1=by_half(tiles["a", j][:].rearrange("p g d -> p (g d)"))[:, u, unit_first:unit_end, :],
                 op0=ALU.mult,
                 op1=ALU.add,
             )
@@ -205,53 +212,39 @@ def tile_block_pb_k_kernel(tc, attn_out, v, x, wo_words, wo_scales, attn_scale, 
             if not in_range(j):
                 return
             if g == POOL_HEAD:
-                shift = work.tile([P, HEAD_DIM], F32, name="shift", tag="shift%d" % g)
-                nc.scalar.activation(
-                    out=laid(shift[:]), in_=by_half(tiles["v", j][:]), func=ACT.Copy, scale=tiles["neg_c%d" % g, j][:, 0:1]
-                )
-            else:
-                shift = work.tile([P, HALF], F32, name="shift", tag="shift%d" % g)
-                nc.scalar.activation(
-                    out=shift[:].rearrange("p (q e) -> p q e", e=PAIR),
-                    in_=by_half(tiles["v", j][:])[:, 1],
-                    func=ACT.Copy,
-                    scale=tiles["neg_c%d" % g, j][:, 0:1],
-                )
-            tiles["shift%d" % g, j] = shift
+                tiles["shift", j] = work.tile([P, PACK * (UNIT_Q - VECTOR_Q)], F32, name="shift", tag="shift")
+            q_first = VECTOR_Q if g == SHARED_HEAD else 0
+            nc.scalar.activation(
+                out=laid(tiles["shift", j][:])[:, :, g * HEAD_Q + q_first - VECTOR_Q : (g + 1) * HEAD_Q - VECTOR_Q, :],
+                in_=by_half(tiles["v", j][:])[:, :, q_first:HEAD_Q, :],
+                func=ACT.Copy,
+                scale=tiles["neg_c%d" % g, j][:, 0:1],
+            )
 
-        def add(j, g):
+        def add(j):
             if not in_range(j):
                 return
-            if g == POOL_HEAD:
-                new_y(j, g)
-                nc.gpsimd.tensor_tensor(
-                    out=laid(tiles["y%d" % g, j][:]),
-                    in0=by_half(tiles["a", j][:, g, :]),
-                    in1=laid(tiles["shift%d" % g, j][:]),
-                    op=ALU.add,
-                )
-            else:
-                new_y(j, g)
-                nc.gpsimd.tensor_tensor(
-                    out=laid(tiles["y%d" % g, j][:])[:, 1],
-                    in0=by_half(tiles["a", j][:, g, :])[:, 1],
-                    in1=tiles["shift%d" % g, j][:].rearrange("p (q e) -> p q e", e=PAIR),
-                    op=ALU.add,
-                )
+            new_y(j)
+            nc.gpsimd.tensor_tensor(
+                out=laid(tiles["y_rest", j][:]),
+                in0=by_half(tiles["a", j][:].rearrange("p g d -> p (g d)"))[:, :, VECTOR_Q:UNIT_Q, :],
+                in1=laid(tiles["shift", j][:]),
+                op=ALU.add,
+            )
 
         def turn(j, g):
             if not in_range(j):
                 return
-            y_words = tiles["y%d" % g, j][:].bitcast(F32)
             turned = psum_t.tile([P, HALVES, HEAD_PASSES * P], F32, name="turned", tag="turned%d" % g)
-            pass_words = K_PASS // PAIR
             for u in range(HALVES):
                 for c in range(HEAD_PASSES):
-                    if PERMUTE:
-                        first = u * (HEAD_PASSES * P) + c * P
-                        words = y_words[:, first : first + P]
+                    q_first = (g * HEAD_PASSES + c) * P
+                    if q_first < VECTOR_Q:
+                        first = u * VECTOR_Q + q_first
+                        words = tiles["y_first", j][:].bitcast(F32)[:, first : first + P]
                     else:
-                        words = y_words[:, c * pass_words + u : (c + 1) * pass_words : HALVES]
+                        first = u * (UNIT_Q - VECTOR_Q) + q_first - VECTOR_Q
+                        words = tiles["y_rest", j][:].bitcast(F32)[:, first : first + P]
                     nc.tensor.transpose(turned[:, u, c * P : (c + 1) * P], words, identity[:])
             tiles["turned%d" % g, j] = turned
 
@@ -348,10 +341,9 @@ def tile_block_pb_k_kernel(tc, attn_out, v, x, wo_words, wo_scales, attn_scale, 
             if s < LAST:
                 scale(s, POOL_HEAD)
             dot(s, SHARED_HEAD)
-            scale(s, SHARED_HEAD)
-            add(s, SHARED_HEAD)
             if s < LAST:
-                add(s, POOL_HEAD)
+                scale(s, SHARED_HEAD)
+                add(s)
             if s == 0:
                 clamp(1)
             invert(s + 1)
@@ -360,27 +352,25 @@ def tile_block_pb_k_kernel(tc, attn_out, v, x, wo_words, wo_scales, attn_scale, 
             if piece == 1:
                 mirror_x(done)
             finish_piece(done, piece)
+            turn(s - 1, SHARED_HEAD)
+            turn(s - 1, POOL_HEAD)
             regroup(s - 1, SHARED_HEAD, True)
             square_sum(s + 3)
-            if s == LAST:
-                multiply(s - 2, BOTH, True, True, (0,))
-                turn(s - 1, POOL_HEAD)
-                multiply(s - 2, BOTH, True, True, (1,))
-            else:
-                turn(s - 1, POOL_HEAD)
-                multiply(s - 2, BOTH, True, True)
+            multiply(s - 2, BOTH, True, True)
             regroup(s - 1, POOL_HEAD, False)
             if s < LAST:
-                subtract(s, SHARED_HEAD, 0)
+                subtract(s, SHARED_HEAD, 0, 0, VECTOR_Q)
+                subtract(s, SHARED_HEAD, 1, 0, VECTOR_Q)
                 mirror(s + 2)
-                turn(s, SHARED_HEAD)
 
-        new_y(LAST, POOL_HEAD)
-        subtract(LAST, POOL_HEAD, 0)
-        subtract(LAST, POOL_HEAD, 1)
+        new_y(LAST)
+        subtract(LAST, POOL_HEAD, 0, 0, HEAD_Q)
+        subtract(LAST, POOL_HEAD, 1, 0, HEAD_Q)
         turn(LAST, POOL_HEAD)
         regroup(LAST, POOL_HEAD, True)
-        subtract(LAST, SHARED_HEAD, 0)
+        for u in range(HALVES):
+            subtract(LAST, SHARED_HEAD, u, 0, VECTOR_Q)
+            subtract(LAST, SHARED_HEAD, u, VECTOR_Q, HEAD_Q)
         quantise(LAST - 1, BOTH)
         turn(LAST, SHARED_HEAD)
         regroup(LAST, SHARED_HEAD, False)

@@ -36,6 +36,7 @@ LIVE_ROWS = 4
 TOKEN_TILES = TOKENS // P
 UNITS = TOKEN_TILES * KV_HEADS
 LOOKAHEAD = 4
+A_AHEAD = 2
 SHARED_HEAD = 0
 POOL_HEAD = 1
 HEAD_Q = HEAD_DIM // PACK
@@ -51,6 +52,7 @@ def tile_block_pb_k_kernel(tc, attn_out, v, x, wo_words, wo_scales, attn_scale, 
     with ExitStack() as ctx:
         consts = ctx.enter_context(tc.tile_pool(name="consts", bufs=1))
         inputs = ctx.enter_context(tc.tile_pool(name="inputs", bufs=LOOKAHEAD + 2))
+        inputs_a = ctx.enter_context(tc.tile_pool(name="inputs_a", bufs=A_AHEAD + 2))
         work = ctx.enter_context(tc.tile_pool(name="work", bufs=2))
         deep = ctx.enter_context(tc.tile_pool(name="deep", bufs=3))
         codes = ctx.enter_context(tc.tile_pool(name="codes", bufs=4))
@@ -96,18 +98,22 @@ def tile_block_pb_k_kernel(tc, attn_out, v, x, wo_words, wo_scales, attn_scale, 
                     in_=wo_scales[passes, rows, :].rearrange("c r n -> r c n").bitcast(I32),
                 )
 
-        def load(j):
+        def load_v(j):
             if not in_range(j):
                 return
             i, h = divmod(j, KV_HEADS)
-            tokens = slice(i * P, (i + 1) * P)
             v_sb = inputs.tile([P, HEAD_DIM], BF16, name="v_sb", tag="v_sb")
-            nc.sync.dma_start(out=v_sb[:], in_=v[0, h, tokens, :])
-            a_sb = inputs.tile([P, GROUP, HEAD_DIM], BF16, name="a_sb", tag="a_sb")
-            nc.sync.dma_start(
-                out=a_sb[:], in_=attn_out[0, h, :, tokens, :].rearrange("g p d -> p g d")
-            )
+            nc.sync.dma_start(out=v_sb[:], in_=v[0, h, i * P : (i + 1) * P, :])
             tiles["v", j] = v_sb
+
+        def load_a(j):
+            if not in_range(j):
+                return
+            i, h = divmod(j, KV_HEADS)
+            a_sb = inputs_a.tile([P, GROUP, HEAD_DIM], BF16, name="a_sb", tag="a_sb")
+            nc.sync.dma_start(
+                out=a_sb[:], in_=attn_out[0, h, :, i * P : (i + 1) * P, :].rearrange("g p d -> p g d")
+            )
             tiles["a", j] = a_sb
 
         def load_x(i):
@@ -314,8 +320,12 @@ def tile_block_pb_k_kernel(tc, attn_out, v, x, wo_words, wo_scales, attn_scale, 
                 )
                 nc.sync.dma_start(out=out[0, i * P : (i + 1) * P, cols], in_=tiles["result", i][:, cols])
 
-        for j in range(LOOKAHEAD):
-            load(j)
+        load_v(0)
+        load_a(0)
+        load_v(1)
+        load_v(2)
+        load_a(1)
+        load_v(3)
         square_sum(0)
         mirror(0)
         clamp(0)
@@ -327,7 +337,8 @@ def tile_block_pb_k_kernel(tc, attn_out, v, x, wo_words, wo_scales, attn_scale, 
         BOTH = (SHARED_HEAD, POOL_HEAD)
         LAST = UNITS - 1
         for s in range(UNITS):
-            load(s + LOOKAHEAD)
+            load_v(s + LOOKAHEAD)
+            load_a(s + A_AHEAD)
             if s < KV_HEADS:
                 load_weights(s)
             elif s == KV_HEADS:

@@ -37,6 +37,9 @@ TOKEN_TILES = TOKENS // P
 UNITS = TOKEN_TILES * KV_HEADS
 LOOKAHEAD = 4
 A_AHEAD = 2
+FIRST_PASSES = 3
+W_LATER = 1
+CATCH_UP = 10
 SHARED_HEAD = 0
 POOL_HEAD = 1
 HEAD_Q = HEAD_DIM // PACK
@@ -280,27 +283,58 @@ def tile_block_pb_k_kernel(tc, attn_out, v, x, wo_words, wo_scales, attn_scale, 
                 in_=tiles["grouped", j][:].rearrange("p g c -> p (g c)")[:, PACK * first : PACK * (first + width)],
             )
 
-        def multiply(j, heads, opens, closes, banks=(0, 1)):
+        pending = []
+        closed = {}
+        emptied = set()
+
+        def enqueue(j, heads):
             if not in_range(j):
                 return
-            i, h = divmod(j, KV_HEADS)
-            if h == 0 and opens and banks[0] == 0:
-                for b in range(N_BANKS):
+            for b in range(N_BANKS):
+                for g in heads:
+                    for c in range(HEAD_PASSES):
+                        pending.append((j, b, g * HEAD_PASSES + c))
+
+        def issue(limit, step):
+            for n in range(min(limit, len(pending))):
+                j, b, c = pending[0]
+                i, h = divmod(j, KV_HEADS)
+                if ("acc%d" % b, i) not in tiles:
+                    if b == 1 and i > 0 and (i - 1, 0) not in emptied:
+                        return
                     tiles["acc%d" % b, i] = psum_acc.tile([P, N_BANK], F32, name="acc", tag="acc")
-            unit_passes = [g * HEAD_PASSES + c for g in heads for c in range(HEAD_PASSES)]
-            for b in banks:
-                for c in unit_passes:
-                    w_pass = h * UNIT_PASSES + c
-                    token_cols = slice(c * P, (c + 1) * P)
-                    nc.tensor.matmul_mx(
-                        out=tiles["acc%d" % b, i][:],
-                        lhsT=tiles["y_codes", j][:, token_cols].bitcast(FP8X4),
-                        lhsT_scale=tiles["y_planes", j][:, token_cols],
-                        rhs=w_words[:, w_pass, b * PAIR * N_BANK : (b + 1) * PAIR * N_BANK].bitcast(FP4X4),
-                        rhs_scale=w_planes[:, w_pass, b * N_BANK : (b + 1) * N_BANK],
-                        start=(h == 0 and opens and c == unit_passes[0]),
-                        stop=(h == KV_HEADS - 1 and closes and c == unit_passes[-1]),
-                    )
+                pending.remove(pending[0])
+                seen[i, b] = seen.get((i, b), 0) + 1
+                w_pass = h * UNIT_PASSES + c
+                token_cols = slice(c * P, (c + 1) * P)
+                nc.tensor.matmul_mx(
+                    out=tiles["acc%d" % b, i][:],
+                    lhsT=tiles["y_codes", j][:, token_cols].bitcast(FP8X4),
+                    lhsT_scale=tiles["y_planes", j][:, token_cols],
+                    rhs=w_words[:, w_pass, b * PAIR * N_BANK : (b + 1) * PAIR * N_BANK].bitcast(FP4X4),
+                    rhs_scale=w_planes[:, w_pass, b * N_BANK : (b + 1) * N_BANK],
+                    start=(seen[i, b] == 1),
+                    stop=(seen[i, b] == PASSES),
+                )
+                if seen[i, b] == PASSES:
+                    closed[i, b] = step
+
+        seen = {}
+        pieces = [(i, piece) for i in range(TOKEN_TILES) for piece in range(4)]
+
+        def finish_next(step):
+            if not pieces:
+                return False
+            i, piece = pieces[0]
+            if piece < N_BANKS and closed.get((i, piece), step) >= step:
+                return False
+            pieces.remove(pieces[0])
+            if piece == 1 and i < TOKEN_TILES - 1:
+                mirror_x(i)
+            finish_piece(i, piece)
+            if piece < N_BANKS:
+                emptied.add((i, piece))
+            return True
 
         def finish_piece(i, piece):
             if not 0 <= i < TOKEN_TILES:
@@ -339,15 +373,14 @@ def tile_block_pb_k_kernel(tc, attn_out, v, x, wo_words, wo_scales, attn_scale, 
         for s in range(UNITS):
             load_v(s + LOOKAHEAD)
             load_a(s + A_AHEAD)
-            if s < KV_HEADS:
-                load_weights(s)
-            elif s == KV_HEADS:
+            if 0 <= s - W_LATER < KV_HEADS:
+                load_weights(s - W_LATER)
+            elif s == KV_HEADS + W_LATER:
                 nc.sync.dma_start(out=gain[:], in_=attn_scale.partition_broadcast(P))
             if s % KV_HEADS == 1:
                 load_x(s // KV_HEADS - 1)
             if s == LAST:
                 load_x(TOKEN_TILES - 1)
-            done, piece = divmod(s - 2 - KV_HEADS, KV_HEADS)
             dot(s, POOL_HEAD)
             if s < LAST:
                 scale(s, POOL_HEAD)
@@ -360,14 +393,15 @@ def tile_block_pb_k_kernel(tc, attn_out, v, x, wo_words, wo_scales, attn_scale, 
             invert(s + 1)
             clamp(s + 2)
             quantise(s - 2, BOTH)
-            if piece == 1:
-                mirror_x(done)
-            finish_piece(done, piece)
+            enqueue(s - 2, BOTH)
+            finish_next(s)
+            if len([k for k in pieces if closed.get((k[0], 1), s) < s]) > 3:
+                finish_next(s)
             turn(s - 1, SHARED_HEAD)
             turn(s - 1, POOL_HEAD)
             regroup(s - 1, SHARED_HEAD, True)
             square_sum(s + 3)
-            multiply(s - 2, BOTH, True, True)
+            issue(0 if s < FIRST_PASSES else UNIT_PASSES * N_BANKS if s < FIRST_PASSES + KV_HEADS else CATCH_UP, s)
             regroup(s - 1, POOL_HEAD, False)
             if s < LAST:
                 subtract(s, SHARED_HEAD, 0, 0, VECTOR_Q)
@@ -383,14 +417,17 @@ def tile_block_pb_k_kernel(tc, attn_out, v, x, wo_words, wo_scales, attn_scale, 
             subtract(LAST, SHARED_HEAD, u, 0, VECTOR_Q)
             subtract(LAST, SHARED_HEAD, u, VECTOR_Q, HEAD_Q)
         quantise(LAST - 1, BOTH)
+        enqueue(LAST - 1, BOTH)
         turn(LAST, SHARED_HEAD)
         regroup(LAST, SHARED_HEAD, False)
-        multiply(LAST - 1, BOTH, True, True)
-        finish_piece(TOKEN_TILES - 2, 2)
-        finish_piece(TOKEN_TILES - 2, 3)
+        issue(len(pending), UNITS)
+        while pieces[0][0] < TOKEN_TILES - 1:
+            finish_next(UNITS + 1)
         quantise(LAST, (POOL_HEAD,))
-        multiply(LAST, (POOL_HEAD,), True, False)
+        enqueue(LAST, (POOL_HEAD,))
+        issue(len(pending), UNITS + 1)
         quantise(LAST, (SHARED_HEAD,))
-        multiply(LAST, (SHARED_HEAD,), False, True)
-        for piece in range(4):
-            finish_piece(TOKEN_TILES - 1, piece)
+        enqueue(LAST, (SHARED_HEAD,))
+        issue(len(pending), UNITS + 1)
+        while pieces:
+            finish_next(UNITS + 2)

from contextlib import ExitStack

import concourse.mybir as mybir
from concourse.masks import make_identity

BF16 = mybir.dt.bfloat16
F32 = mybir.dt.float32
I32 = mybir.dt.int32
U32 = mybir.dt.uint32
U8 = mybir.dt.uint8
FP8X4 = mybir.dt.float8_e4m3fn_x4
FP4X4 = mybir.dt.float4_e2m1fn_x4
ALU = mybir.AluOpType
ACT = mybir.ActivationFunctionType

P = 128
TOKENS = 640
KV_HEADS = 4
GROUP = 2
HEAD_DIM = 1024
D_OUT = 1024
NORM_FLOOR = 1e-12

PACK = 4
K_PASS = P * PACK
HEAD_PASSES = HEAD_DIM // K_PASS
UNIT_PASSES = GROUP * HEAD_PASSES
PASSES = KV_HEADS * UNIT_PASSES
N_BANK = 512
N_BANKS = D_OUT // N_BANK
PAIR = 2
HALVES = PACK // PAIR
QUADRANTS = 4
LIVE_ROWS = 4

TOKEN_TILES = TOKENS // P
UNITS = TOKEN_TILES * KV_HEADS
LOOKAHEAD = 4
A_AHEAD = 2
FIRST_PASSES = 3
W_LATER = 1
CATCH_UP = 10
SHARED_HEAD = 0
POOL_HEAD = 1
HEAD_Q = HEAD_DIM // PACK
UNIT_Q = GROUP * HEAD_Q
VECTOR_Q = 128
HALF = HEAD_DIM // 2

FLOPS = 2 * TOKENS * KV_HEADS * GROUP * HEAD_DIM * D_OUT


def tile_block_pb_k_kernel(tc, attn_out, v, x, wo_words, wo_scales, attn_scale, out):
    nc = tc.nc
    with ExitStack() as ctx:
        consts = ctx.enter_context(tc.tile_pool(name="consts", bufs=1))
        inputs = ctx.enter_context(tc.tile_pool(name="inputs", bufs=LOOKAHEAD + 2))
        inputs_a = ctx.enter_context(tc.tile_pool(name="inputs_a", bufs=A_AHEAD + 2))
        work = ctx.enter_context(tc.tile_pool(name="work", bufs=2))
        deep = ctx.enter_context(tc.tile_pool(name="deep", bufs=3))
        codes = ctx.enter_context(tc.tile_pool(name="codes", bufs=4))
        small = ctx.enter_context(tc.tile_pool(name="small", bufs=4))
        psum_v = ctx.enter_context(tc.psum_pool(name="psum_v", bufs=2))
        psum_t = ctx.enter_context(tc.psum_pool(name="psum_t", bufs=1))
        psum_acc = ctx.enter_context(tc.psum_pool(name="psum_acc", bufs=3))
        psum_x = ctx.enter_context(tc.psum_pool(name="psum_x", bufs=1))
        ctx.enter_context(tc.manual_schedule())

        tiles = {}

        identity = consts.tile([P, P], F32, name="identity")
        make_identity(nc, identity[:])
        identity_bf = consts.tile([P, P], BF16, name="identity_bf")
        make_identity(nc, identity_bf[:])

        w_words = consts.tile([P, PASSES, PAIR * D_OUT], U8, name="w_words", align_bytes=64)
        w_planes = consts.tile([P, PASSES, D_OUT], U8, name="w_planes", align_bytes=64)
        nc.vector.memset(w_planes[:].bitcast(I32), 0)
        gain = consts.tile([P, D_OUT], BF16, name="gain")

        def in_range(j):
            return 0 <= j < UNITS

        def by_half(ap):
            return ap.rearrange("p (q u e) -> p u q e", u=HALVES, e=PAIR)

        def laid(ap):
            return ap.rearrange("p (u q e) -> p u q e", u=HALVES, e=PAIR)

        def load_weights(h):
            passes = slice(h * UNIT_PASSES, (h + 1) * UNIT_PASSES)
            nc.sync.dma_start(
                out=w_words[:, passes, :].bitcast(I32),
                in_=wo_words[passes].rearrange("c p b -> p c b").bitcast(I32),
            )
            for quadrant in range(QUADRANTS):
                rows = slice(quadrant * LIVE_ROWS, (quadrant + 1) * LIVE_ROWS)
                first = quadrant * (P // QUADRANTS)
                nc.sync.dma_start(
                    out=w_planes[first : first + LIVE_ROWS, passes, :].bitcast(I32),
                    in_=wo_scales[passes, rows, :].rearrange("c r n -> r c n").bitcast(I32),
                )

        def load_v(j):
            if not in_range(j):
                return
            i, h = divmod(j, KV_HEADS)
            v_sb = inputs.tile([P, HEAD_DIM], BF16, name="v_sb", tag="v_sb")
            nc.sync.dma_start(out=v_sb[:], in_=v[0, h, i * P : (i + 1) * P, :])
            tiles["v", j] = v_sb

        def load_a(j):
            if not in_range(j):
                return
            i, h = divmod(j, KV_HEADS)
            a_sb = inputs_a.tile([P, GROUP, HEAD_DIM], BF16, name="a_sb", tag="a_sb")
            nc.sync.dma_start(
                out=a_sb[:], in_=attn_out[0, h, :, i * P : (i + 1) * P, :].rearrange("g p d -> p g d")
            )
            tiles["a", j] = a_sb

        def load_x(i):
            if not 0 <= i < TOKEN_TILES:
                return
            x_sb = work.tile([P, D_OUT], BF16, name="x_sb", tag="x_sb")
            nc.sync.dma_start(out=x_sb[:], in_=x[0, i * P : (i + 1) * P, :])
            tiles["x", i] = x_sb

        def square_sum(j):
            if not in_range(j):
                return
            squares = work.tile([P, HEAD_DIM], BF16, name="squares", tag="squares")
            ssq = small.tile([P, 1], F32, name="ssq", tag="ssq")
            nc.scalar.activation(
                out=squares[:], in_=tiles["v", j][:], func=ACT.Square, accum_out=ssq[:]
            )
            tiles["ssq", j] = ssq

        def mirror(j):
            if not in_range(j):
                return
            v_ps = psum_v.tile([P, HEAD_DIM], BF16, name="v_ps", tag="v_ps")
            for b in range(HEAD_DIM // N_BANK):
                cols = slice(b * N_BANK, (b + 1) * N_BANK)
                nc.tensor.matmul(
                    out=v_ps[:, cols], lhsT=identity_bf[:], rhs=tiles["v", j][:, cols], start=True, stop=True
                )
            tiles["v_ps", j] = v_ps

        def mirror_x(i):
            if not 0 <= i < TOKEN_TILES:
                return
            x_ps = psum_x.tile([P, D_OUT], BF16, name="x_ps", tag="x_ps")
            for b in range(N_BANKS):
                cols = slice(b * N_BANK, (b + 1) * N_BANK)
                nc.tensor.matmul(
                    out=x_ps[:, cols], lhsT=identity_bf[:], rhs=tiles["x", i][:, cols], start=True, stop=True
                )
            tiles["x_ps", i] = x_ps

        def clamp(j):
            if not in_range(j):
                return
            neg_ssq = small.tile([P, 1], F32, name="neg_ssq", tag="neg_ssq")
            nc.vector.tensor_scalar(
                out=neg_ssq[:],
                in0=tiles["ssq", j][:],
                scalar1=NORM_FLOOR * NORM_FLOOR,
                scalar2=-1.0,
                op0=ALU.max,
                op1=ALU.mult,
            )
            tiles["neg_ssq", j] = neg_ssq

        def invert(j):
            if not in_range(j):
                return
            neg_inv = small.tile([P, 1], F32, name="neg_inv", tag="neg_inv")
            nc.vector.reciprocal(out=neg_inv[:], in_=tiles["neg_ssq", j][:])
            tiles["neg_inv", j] = neg_inv

        def dot(j, g):
            if not in_range(j):
                return
            neg_c = small.tile([P, 1], F32, name="neg_c", tag="neg_c%d" % g)
            tiles["neg_c%d" % g, j] = neg_c
            products = work.tile([P, HEAD_DIM], BF16, name="products", tag="products")
            nc.vector.scalar_tensor_tensor(
                out=products[:],
                in0=tiles["a", j][:, g, :],
                scalar=tiles["neg_inv", j][:, 0:1],
                in1=tiles["v_ps", j][:],
                op0=ALU.mult,
                op1=ALU.mult,
                accum_out=neg_c[:],
            )

        def new_y(j):
            tiles["y_first", j] = deep.tile([P, PACK * VECTOR_Q], BF16, name="y_first", tag="y_first")
            tiles["y_rest", j] = deep.tile([P, PACK * (UNIT_Q - VECTOR_Q)], BF16, name="y_rest", tag="y_rest")

        def subtract(j, g, u, q_first, q_end):
            if not in_range(j):
                return
            unit_first = g * HEAD_Q + q_first
            unit_end = g * HEAD_Q + q_end
            if unit_end <= VECTOR_Q:
                y_part = laid(tiles["y_first", j][:])[:, u, unit_first:unit_end, :]
            else:
                y_part = laid(tiles["y_rest", j][:])[:, u, unit_first - VECTOR_Q : unit_end - VECTOR_Q, :]
            nc.vector.scalar_tensor_tensor(
                out=y_part,
                in0=by_half(tiles["v_ps", j][:])[:, u, q_first:q_end, :],
                scalar=tiles["neg_c%d" % g, j][:, 0:1],
                in1=by_half(tiles["a", j][:].rearrange("p g d -> p (g d)"))[:, u, unit_first:unit_end, :],
                op0=ALU.mult,
                op1=ALU.add,
            )

        def scale(j, g):
            if not in_range(j):
                return
            if g == POOL_HEAD:
                tiles["shift", j] = work.tile([P, PACK * (UNIT_Q - VECTOR_Q)], F32, name="shift", tag="shift")
            q_first = VECTOR_Q if g == SHARED_HEAD else 0
            nc.scalar.activation(
                out=laid(tiles["shift", j][:])[:, :, g * HEAD_Q + q_first - VECTOR_Q : (g + 1) * HEAD_Q - VECTOR_Q, :],
                in_=by_half(tiles["v", j][:])[:, :, q_first:HEAD_Q, :],
                func=ACT.Copy,
                scale=tiles["neg_c%d" % g, j][:, 0:1],
            )

        def add(j):
            if not in_range(j):
                return
            new_y(j)
            nc.gpsimd.tensor_tensor(
                out=laid(tiles["y_rest", j][:]),
                in0=by_half(tiles["a", j][:].rearrange("p g d -> p (g d)"))[:, :, VECTOR_Q:UNIT_Q, :],
                in1=laid(tiles["shift", j][:]),
                op=ALU.add,
            )

        def turn(j, g):
            if not in_range(j):
                return
            turned = psum_t.tile([P, HALVES, HEAD_PASSES * P], F32, name="turned", tag="turned%d" % g)
            for u in range(HALVES):
                for c in range(HEAD_PASSES):
                    q_first = (g * HEAD_PASSES + c) * P
                    if q_first < VECTOR_Q:
                        first = u * VECTOR_Q + q_first
                        words = tiles["y_first", j][:].bitcast(F32)[:, first : first + P]
                    else:
                        first = u * (UNIT_Q - VECTOR_Q) + q_first - VECTOR_Q
                        words = tiles["y_rest", j][:].bitcast(F32)[:, first : first + P]
                    nc.tensor.transpose(turned[:, u, c * P : (c + 1) * P], words, identity[:])
            tiles["turned%d" % g, j] = turned

        def regroup(j, g, first):
            if not in_range(j):
                return
            if first:
                tiles["grouped", j] = work.tile(
                    [P, GROUP, PACK * HEAD_PASSES * P], BF16, name="grouped", tag="grouped", align_bytes=64
                )
            nc.scalar.copy(
                out=tiles["grouped", j][:, g, :].bitcast(F32).rearrange("p (q u) -> p q u", u=HALVES),
                in_=tiles["turned%d" % g, j][:].rearrange("p u q -> p q u"),
            )

        def quantise(j, heads):
            if not in_range(j):
                return
            if ("y_codes", j) not in tiles:
                tiles["y_codes", j] = codes.tile([P, UNIT_PASSES * P], U32, name="y_codes", tag="y_codes", align_bytes=64)
                tiles["y_planes", j] = codes.tile([P, UNIT_PASSES * P], U8, name="y_planes", tag="y_planes", align_bytes=64)
            first = min(heads) * HEAD_PASSES * P
            width = len(heads) * HEAD_PASSES * P
            nc.vector.quantize_mx(
                out=tiles["y_codes", j][:, first : first + width].bitcast(FP8X4),
                scales=tiles["y_planes", j][:, first : first + width],
                in_=tiles["grouped", j][:].rearrange("p g c -> p (g c)")[:, PACK * first : PACK * (first + width)],
            )

        pending = []
        closed = {}
        emptied = set()

        def enqueue(j, heads):
            if not in_range(j):
                return
            for b in range(N_BANKS):
                for g in heads:
                    for c in range(HEAD_PASSES):
                        pending.append((j, b, g * HEAD_PASSES + c))

        def issue(limit, step):
            for n in range(min(limit, len(pending))):
                j, b, c = pending[0]
                i, h = divmod(j, KV_HEADS)
                if ("acc%d" % b, i) not in tiles:
                    if b == 1 and i > 0 and (i - 1, 0) not in emptied:
                        return
                    tiles["acc%d" % b, i] = psum_acc.tile([P, N_BANK], F32, name="acc", tag="acc")
                pending.remove(pending[0])
                seen[i, b] = seen.get((i, b), 0) + 1
                w_pass = h * UNIT_PASSES + c
                token_cols = slice(c * P, (c + 1) * P)
                nc.tensor.matmul_mx(
                    out=tiles["acc%d" % b, i][:],
                    lhsT=tiles["y_codes", j][:, token_cols].bitcast(FP8X4),
                    lhsT_scale=tiles["y_planes", j][:, token_cols],
                    rhs=w_words[:, w_pass, b * PAIR * N_BANK : (b + 1) * PAIR * N_BANK].bitcast(FP4X4),
                    rhs_scale=w_planes[:, w_pass, b * N_BANK : (b + 1) * N_BANK],
                    start=(seen[i, b] == 1),
                    stop=(seen[i, b] == PASSES),
                )
                if seen[i, b] == PASSES:
                    closed[i, b] = step

        seen = {}
        pieces = [(i, piece) for i in range(TOKEN_TILES) for piece in range(4)]

        def finish_next(step):
            if not pieces:
                return False
            i, piece = pieces[0]
            if piece < N_BANKS and closed.get((i, piece), step) >= step:
                return False
            pieces.remove(pieces[0])
            if piece == 1 and i < TOKEN_TILES - 1:
                mirror_x(i)
            finish_piece(i, piece)
            if piece < N_BANKS:
                emptied.add((i, piece))
            return True

        def finish_piece(i, piece):
            if not 0 <= i < TOKEN_TILES:
                return
            b = piece % N_BANKS
            cols = slice(b * N_BANK, (b + 1) * N_BANK)
            if piece == 0:
                tiles["scaled", i] = work.tile([P, D_OUT], F32, name="scaled", tag="scaled")
                tiles["result", i] = work.tile([P, D_OUT], F32, name="result", tag="result")
            if piece < N_BANKS:
                nc.vector.tensor_tensor(
                    out=tiles["scaled", i][:, cols], in0=tiles["acc%d" % b, i][:], in1=gain[:, cols], op=ALU.mult
                )
            else:
                nc.vector.tensor_tensor(
                    out=tiles["result", i][:, cols], in0=tiles["scaled", i][:, cols], in1=tiles.get(("x_ps", i), tiles["x", i])[:, cols], op=ALU.add
                )
                nc.sync.dma_start(out=out[0, i * P : (i + 1) * P, cols], in_=tiles["result", i][:, cols])

        load_v(0)
        load_a(0)
        load_v(1)
        load_v(2)
        load_a(1)
        load_v(3)
        square_sum(0)
        mirror(0)
        clamp(0)
        invert(0)
        square_sum(1)
        mirror(1)
        square_sum(2)

        BOTH = (SHARED_HEAD, POOL_HEAD)
        LAST = UNITS - 1
        for s in range(UNITS):
            load_v(s + LOOKAHEAD)
            load_a(s + A_AHEAD)
            if 0 <= s - W_LATER < KV_HEADS:
                load_weights(s - W_LATER)
            elif s == KV_HEADS + W_LATER:
                nc.sync.dma_start(out=gain[:], in_=attn_scale.partition_broadcast(P))
            if s % KV_HEADS == 1:
                load_x(s // KV_HEADS - 1)
            if s == LAST:
                load_x(TOKEN_TILES - 1)
            dot(s, POOL_HEAD)
            if s < LAST:
                scale(s, POOL_HEAD)
            dot(s, SHARED_HEAD)
            if s < LAST:
                scale(s, SHARED_HEAD)
                add(s)
            if s == 0:
                clamp(1)
            invert(s + 1)
            clamp(s + 2)
            quantise(s - 2, BOTH)
            enqueue(s - 2, BOTH)
            finish_next(s)
            if len([k for k in pieces if closed.get((k[0], 1), s) < s]) > 3:
                finish_next(s)
            turn(s - 1, SHARED_HEAD)
            turn(s - 1, POOL_HEAD)
            regroup(s - 1, SHARED_HEAD, True)
            square_sum(s + 3)
            issue(0 if s < FIRST_PASSES else UNIT_PASSES * N_BANKS if s < FIRST_PASSES + KV_HEADS else CATCH_UP, s)
            regroup(s - 1, POOL_HEAD, False)
            if s < LAST:
                subtract(s, SHARED_HEAD, 0, 0, VECTOR_Q)
                subtract(s, SHARED_HEAD, 1, 0, VECTOR_Q)
                mirror(s + 2)

        new_y(LAST)
        subtract(LAST, POOL_HEAD, 0, 0, HEAD_Q)
        subtract(LAST, POOL_HEAD, 1, 0, HEAD_Q)
        turn(LAST, POOL_HEAD)
        regroup(LAST, POOL_HEAD, True)
        for u in range(HALVES):
            subtract(LAST, SHARED_HEAD, u, 0, VECTOR_Q)
            subtract(LAST, SHARED_HEAD, u, VECTOR_Q, HEAD_Q)
        quantise(LAST - 1, BOTH)
        enqueue(LAST - 1, BOTH)
        turn(LAST, SHARED_HEAD)
        regroup(LAST, SHARED_HEAD, False)
        issue(len(pending), UNITS)
        while pieces[0][0] < TOKEN_TILES - 1:
            finish_next(UNITS + 1)
        quantise(LAST, (POOL_HEAD,))
        enqueue(LAST, (POOL_HEAD,))
        issue(len(pending), UNITS + 1)
        quantise(LAST, (SHARED_HEAD,))
        enqueue(LAST, (SHARED_HEAD,))
        issue(len(pending), UNITS + 1)
        while pieces:
            finish_next(UNITS + 2)
